import numpy as np
import ml_dtypes


def mxq(x, axis, fmt="e4m3"):
    dtype, down = {"e4m3": (ml_dtypes.float8_e4m3fn, 7), "e5m2": (ml_dtypes.float8_e5m2, 14)}[fmt]
    v = np.moveaxis(np.asarray(x, np.float32).astype(ml_dtypes.bfloat16).astype(np.float64), axis, -1)
    blocks = v.reshape(v.shape[:-1] + (-1, 32))
    amax = np.abs(blocks).max(-1, keepdims=True)
    byte = np.maximum(np.where(amax > 0, np.frexp(amax)[1] - 1 + 127, 0) - down, 1)
    scale = np.exp2(byte - 127.0)
    codes = (blocks / scale).astype(np.float32).astype(dtype).astype(np.float64)
    return np.moveaxis((codes * scale).reshape(v.shape), -1, axis)


WIDE = False


def mx_kscale(k):
    if not WIDE:
        return np.ones(k)
    levels = np.array([10, -10, 5, -5, 0])
    a = np.random.permutation(np.resize(levels, k // 512 * 4)).reshape(k // 512, 4)
    idx = np.arange(k)
    return np.exp2(a[idx // 512, idx % 128 // 32])


BF16 = ml_dtypes.bfloat16


def bf(x):
    return np.asarray(x, np.float32).astype(BF16)


def f64(x):
    return np.asarray(x).astype(np.float64)


B, C, H, W, K, M = 8, 1024, 32, 64, 16, 8
D = C
LOG2PI = float(np.log(2.0 * np.pi))


def setup_inputs():
    t = mx_kscale(D)
    a = D ** -0.25
    feats = np.random.standard_normal((B, C, H, W)) * 1.5 * a * t[None, :, None, None]
    means = np.random.standard_normal((K, M, D)) * a * t
    r = np.random.standard_normal((K, M, D)) * 0.5
    log_vars = r - r.mean(-1, keepdims=True) + np.random.standard_normal((K, M, 1)) / D + 2.0 * np.log(t)
    u = np.random.uniform(size=(K, M))
    log_weights = u - np.log(np.exp(u).sum(-1, keepdims=True))
    return {"feats": bf(feats), "means": bf(means), "log_vars": bf(log_vars), "log_weights": bf(log_weights)}


def reference(feats, means, log_vars, log_weights):
    feats, means, log_vars, log_weights = f64(feats), f64(means), f64(log_vars), f64(log_weights)
    x = feats.transpose(0, 2, 3, 1).reshape(-1, C)
    inv_var = np.exp(-log_vars)
    xsq_iv = (mxq(x * x, 1, "e4m3") @ mxq(inv_var.reshape(K * M, D), 1, "e4m3").T).reshape(-1, K, M)
    x_mu_iv = (mxq(x, 1, "e4m3") @ mxq((means * inv_var).reshape(K * M, D), 1, "e4m3").T).reshape(-1, K, M)
    mu_sq_iv = np.sum(means * means * inv_var, axis=-1)
    maha = xsq_iv - 2.0 * x_mu_iv + mu_sq_iv[None]
    log_det = np.sum(log_vars, axis=-1)
    log_prob = -0.5 * (D * LOG2PI + log_det[None] + maha)
    z = log_prob + log_weights[None]
    zm = z.max(-1, keepdims=True)
    log_lik = np.log(np.exp(z - zm).sum(-1)) + zm[..., 0]
    e = np.exp(log_lik - log_lik.max(-1, keepdims=True))
    probs = e / e.sum(-1, keepdims=True)
    anomaly = 1.0 - probs.max(axis=1)
    return anomaly.reshape(B, H, W)

@@ -1,0 +1,187 @@
+from contextlib import ExitStack
+
+import concourse.mybir as mybir
+from concourse.masks import make_identity
+
+F32 = mybir.dt.float32
+BF16 = mybir.dt.bfloat16
+U32 = mybir.dt.uint32
+U8 = mybir.dt.uint8
+FP8X4 = mybir.dt.float8_e4m3fn_x4
+ACT = mybir.ActivationFunctionType
+ALU = mybir.AluOpType
+AX = mybir.AxisListType
+
+P = 128
+PACK = 4
+K_PASS = P * PACK
+B = 8
+D = 1024
+HW = 2048
+G = D // K_PASS
+NLOAD = 1024
+NG = 512
+NT = NG // P
+NCLS = 16
+NCMP = 8
+
+FLOPS = 2 * 2 * (B * HW) * D * P
+
+
+def tile_gmmoutlierdetector_t_kernel(tc, feats, means, log_vars, log_weights, out):
+    nc = tc.nc
+    with ExitStack() as ctx:
+        const = ctx.enter_context(tc.tile_pool(name="const", bufs=1))
+        rawp = ctx.enter_context(tc.tile_pool(name="rawp", bufs=4))
+        work = ctx.enter_context(tc.tile_pool(name="work", bufs=3))
+        ps_acc = ctx.enter_context(tc.psum_pool(name="ps_acc", bufs=2))
+        ps_t = ctx.enter_context(tc.psum_pool(name="ps_t", bufs=4))
+        ps_w = ctx.enter_context(tc.psum_pool(name="ps_w", bufs=2))
+
+        fv = feats.rearrange("b (g p t) h w -> b g p t (h w)", g=G, p=P, t=PACK)
+
+        lv = const.tile([P, D], BF16, name="lv")
+        mu = const.tile([P, D], BF16, name="mu")
+        lw = const.tile([P, 1], BF16, name="lw")
+        nc.scalar.dma_start(out=lv[:], in_=log_vars.rearrange("k m d -> (k m) d"))
+        nc.scalar.dma_start(out=mu[:], in_=means.rearrange("k m d -> (k m) d"))
+        with nc.allow_non_contiguous_dma(reason="128 log weights, one to a partition"):
+            nc.scalar.dma_start(out=lw[:], in_=log_weights.rearrange("k (m o) -> (k m) o", o=1))
+
+        ident_bf = const.tile([P, P], BF16, name="ident_bf")
+        make_identity(nc, ident_bf[:])
+        ident_f = const.tile([P, P], F32, name="ident_f")
+        make_identity(nc, ident_f[:])
+        center = const.tile([P, P], BF16, name="center")
+        nc.vector.tensor_scalar(
+            out=center[:], in0=ident_bf[:], scalar1=-1.0 / P, scalar2=None, op0=ALU.add
+        )
+
+        iv32 = const.tile([P, D], F32, name="iv32")
+        nc.scalar.activation(out=iv32[:], in_=lv[:], func=ACT.Exp, scale=-1.0)
+        miv32 = const.tile([P, D], F32, name="miv32")
+        nc.vector.tensor_tensor(out=miv32[:], in0=mu[:], in1=iv32[:], op=ALU.mult)
+        m2iv = const.tile([P, D], F32, name="m2iv")
+        nc.vector.tensor_tensor(out=m2iv[:], in0=mu[:], in1=miv32[:], op=ALU.mult)
+
+        parts = const.tile([P, 3], F32, name="parts")
+        nc.vector.tensor_reduce(out=parts[:, 2:3], in_=m2iv[:], axis=AX.X, op=ALU.add)
+        for h in range(2):
+            ld_ps = ps_w.tile([P, 512], F32, tag="w", name="ld_ps")
+            nc.tensor.matmul(
+                out=ld_ps[:], lhsT=center[:], rhs=lv[:, h * 512 : (h + 1) * 512], start=True, stop=True
+            )
+            nc.vector.tensor_reduce(out=parts[:, h : h + 1], in_=ld_ps[:], axis=AX.X, op=ALU.add)
+        psum3 = const.tile([P, 1], F32, name="psum3")
+        nc.vector.tensor_reduce(out=psum3[:], in_=parts[:], axis=AX.X, op=ALU.add)
+        ybias = const.tile([P, 1], F32, name="ybias")
+        nc.vector.scalar_tensor_tensor(
+            out=ybias[:], in0=psum3[:], scalar=0.5, in1=lw[:], op0=ALU.mult, op1=ALU.subtract
+        )
+
+        wb = const.tile([P, 2, G, PACK, P], BF16, name="wb")
+        nc.vector.tensor_copy(
+            out=wb[:, 0], in_=iv32[:].rearrange("c (g p t) -> c g t p", g=G, p=P, t=PACK)
+        )
+        nc.vector.tensor_scalar(
+            out=wb[:, 1],
+            in0=miv32[:].rearrange("c (g p t) -> c g t p", g=G, p=P, t=PACK),
+            scalar1=-2.0,
+            scalar2=None,
+            op0=ALU.mult,
+        )
+        wg = const.tile([P, 2 * G, P, PACK], BF16, name="wg", align_bytes=64)
+        for o in range(2):
+            for g in range(G):
+                wT = ps_w.tile([P, PACK, P], BF16, tag="w", name="wT")
+                for t in range(PACK):
+                    nc.tensor.transpose(wT[:, t, :], wb[:, o, g, t, :], ident_bf[:])
+                nc.vector.tensor_copy(
+                    out=wg[:, o * G + g], in_=wT[:].rearrange("p t c -> p c t")
+                )
+        wc = const.tile([P, 2 * G * P], U32, name="wc", align_bytes=64)
+        ws = const.tile([P, 2 * G * P], U8, name="ws", align_bytes=64)
+        nc.vector.quantize_mx(
+            out=wc[:].bitcast(FP8X4), scales=ws[:], in_=wg[:].rearrange("p a c t -> p (a c t)")
+        )
+
+        gs_all = const.tile([P, P * NCLS], F32, name="gs_all")
+
+        for b in range(B):
+            for h in range(HW // NLOAD):
+                raw = rawp.tile([P, G, PACK, NLOAD], BF16, tag="raw", name="raw")
+                for g in range(G):
+                    nc.sync.dma_start(
+                        out=raw[:, g], in_=fv[b, g, :, :, h * NLOAD : (h + 1) * NLOAD]
+                    )
+                for q in range(NLOAD // NG):
+                    n0 = q * NG
+                    tile0 = (b * HW + h * NLOAD + n0) // P
+                    xg = work.tile([P, G, NG, PACK], BF16, tag="xg", name="xg", align_bytes=64)
+                    for g in range(G):
+                        nc.vector.tensor_copy(
+                            out=xg[:, g].rearrange("p (c i) t -> p c t i", i=4),
+                            in_=raw[:, g, :, n0 : n0 + NG].rearrange("p t (c i) -> p c t i", i=4),
+                        )
+                    xg_flat = xg[:].rearrange("p g n t -> p (g n t)")
+                    x2 = work.tile([P, G * NG * PACK], BF16, tag="x2", name="x2", align_bytes=64)
+                    nc.scalar.activation(out=x2[:], in_=xg_flat, func=ACT.Square)
+                    xc = work.tile([P, G * NG], U32, tag="xc", name="xc", align_bytes=64)
+                    xs = work.tile([P, G * NG], U8, tag="xs", name="xs", align_bytes=64)
+                    nc.vector.quantize_mx(out=xc[:].bitcast(FP8X4), scales=xs[:], in_=xg_flat)
+                    x2c = work.tile([P, G * NG], U32, tag="x2c", name="x2c", align_bytes=64)
+                    x2s = work.tile([P, G * NG], U8, tag="x2s", name="x2s", align_bytes=64)
+                    nc.vector.quantize_mx(out=x2c[:].bitcast(FP8X4), scales=x2s[:], in_=x2[:])
+
+                    acc = ps_acc.tile([P, NG], F32, tag="acc", name="acc")
+                    passes = [(1, g, xc, xs) for g in range(G)] + [(0, g, x2c, x2s) for g in range(G)]
+                    for idx, (o, g, codes, scales) in enumerate(passes):
+                        a = (o * G + g) * P
+                        nc.tensor.matmul_mx(
+                            out=acc[:],
+                            lhsT=wc[:, a : a + P].bitcast(FP8X4),
+                            lhsT_scale=ws[:, a : a + P],
+                            rhs=codes[:, g * NG : (g + 1) * NG].bitcast(FP8X4),
+                            rhs_scale=scales[:, g * NG : (g + 1) * NG],
+                            start=(idx == 0),
+                            stop=(idx == len(passes) - 1),
+                        )
+                    y = work.tile([P, NG], F32, tag="y", name="y")
+                    nc.scalar.activation(
+                        out=y[:], in_=acc[:], func=ACT.Identity, bias=ybias[:, 0:1], scale=0.5
+                    )
+                    yT = ps_t.tile([P, NT, P], F32, tag="yT", name="yT")
+                    for j in range(NT):
+                        nc.tensor.transpose(yT[:, j, :], y[:, j * P : (j + 1) * P], ident_f[:])
+                    mn = work.tile([P, NT], F32, tag="mn", name="mn")
+                    nc.vector.tensor_reduce(out=mn[:], in_=yT[:], axis=AX.X, op=ALU.min)
+                    e = work.tile([P, NT, P], F32, tag="e", name="e")
+                    for j in range(NT):
+                        nc.scalar.activation(
+                            out=e[:, j, :], in_=yT[:, j, :], func=ACT.Exp, bias=mn[:, j : j + 1], scale=-1.0
+                        )
+                    nc.vector.tensor_reduce(
+                        out=gs_all[:, tile0 * NCLS : (tile0 + NT) * NCLS],
+                        in_=e[:].rearrange("p j (k m) -> p (j k) m", m=NCMP),
+                        axis=AX.X,
+                        op=ALU.add,
+                    )
+
+        gs_v = gs_all[:].rearrange("p (n k) -> p n k", k=NCLS)
+        top = const.tile([P, P], F32, name="top")
+        nc.vector.tensor_reduce(out=top[:], in_=gs_v, axis=AX.X, op=ALU.max)
+        tot = const.tile([P, P], F32, name="tot")
+        nc.vector.tensor_reduce(out=tot[:], in_=gs_v, axis=AX.X, op=ALU.add)
+        rec = const.tile([P, P], F32, name="rec")
+        nc.vector.reciprocal(out=rec[:], in_=tot[:])
+        share = const.tile([P, P], F32, name="share")
+        nc.vector.tensor_tensor(out=share[:], in0=top[:], in1=rec[:], op=ALU.mult)
+        res = const.tile([P, P], F32, name="res")
+        nc.vector.tensor_scalar(
+            out=res[:], in0=share[:], scalar1=-1.0, scalar2=1.0, op0=ALU.mult, op1=ALU.add
+        )
+        resT = ps_w.tile([P, P], F32, tag="w", name="resT")
+        nc.tensor.transpose(resT[:], res[:], ident_f[:])
+        res_sb = const.tile([P, P], F32, name="res_sb")
+        nc.vector.tensor_copy(out=res_sb[:], in_=resT[:])
+        nc.sync.dma_start(out=out.rearrange("b (x y) w -> (b x) (y w)", y=2), in_=res_sb[:])

@@ -24,6 +24,7 @@ NG = 512
 NT = NG // P
 NCLS = 16
 NCMP = 8
+TB = 32
 
 FLOPS = 2 * 2 * (B * HW) * D * P
 
@@ -36,7 +37,7 @@ def tile_gmmoutlierdetector_t_kernel(tc, feats, means, log_vars, log_weights, ou
         work = ctx.enter_context(tc.tile_pool(name="work", bufs=3))
         ps_acc = ctx.enter_context(tc.psum_pool(name="ps_acc", bufs=2))
         ps_t = ctx.enter_context(tc.psum_pool(name="ps_t", bufs=4))
-        ps_w = ctx.enter_context(tc.psum_pool(name="ps_w", bufs=2))
+        ps_s = ctx.enter_context(tc.psum_pool(name="ps_s", bufs=2))
 
         fv = feats.rearrange("b (g p t) h w -> b g p t (h w)", g=G, p=P, t=PACK)
 
@@ -60,18 +61,53 @@ def tile_gmmoutlierdetector_t_kernel(tc, feats, means, log_vars, log_weights, ou
         iv32 = const.tile([P, D], F32, name="iv32")
         nc.scalar.activation(out=iv32[:], in_=lv[:], func=ACT.Exp, scale=-1.0)
         miv32 = const.tile([P, D], F32, name="miv32")
-        nc.vector.tensor_tensor(out=miv32[:], in0=mu[:], in1=iv32[:], op=ALU.mult)
-        m2iv = const.tile([P, D], F32, name="m2iv")
-        nc.vector.tensor_tensor(out=m2iv[:], in0=mu[:], in1=miv32[:], op=ALU.mult)
+        nc.gpsimd.tensor_tensor(out=miv32[:], in0=mu[:], in1=iv32[:], op=ALU.mult)
 
+        wb = const.tile([P, 2, G, PACK, P], BF16, name="wb")
+        nc.gpsimd.tensor_scalar(
+            out=wb[:, 0],
+            in0=iv32[:].rearrange("c (g p t) -> c g t p", g=G, p=P, t=PACK),
+            scalar1=1.0,
+            scalar2=0.0,
+            op0=ALU.mult,
+            op1=ALU.add,
+        )
+        nc.gpsimd.tensor_scalar(
+            out=wb[:, 1],
+            in0=miv32[:].rearrange("c (g p t) -> c g t p", g=G, p=P, t=PACK),
+            scalar1=-2.0,
+            scalar2=0.0,
+            op0=ALU.mult,
+            op1=ALU.add,
+        )
+        wg = const.tile([P, 2 * G, P, PACK], BF16, name="wg", align_bytes=64)
+        for o in range(2):
+            for g in range(G):
+                wT = ps_t.tile([P, PACK, P], BF16, tag="yT", name="wT")
+                for t in range(PACK):
+                    nc.tensor.transpose(wT[:, t, :], wb[:, o, g, t, :], ident_bf[:])
+                nc.scalar.copy(out=wg[:, o * G + g], in_=wT[:].rearrange("p t c -> p c t"))
+        wc = const.tile([P, 2 * G * P], U32, name="wc", align_bytes=64)
+        ws = const.tile([P, 2 * G * P], U8, name="ws", align_bytes=64)
+        nc.vector.quantize_mx(
+            out=wc[:].bitcast(FP8X4), scales=ws[:], in_=wg[:].rearrange("p a c t -> p (a c t)")
+        )
+
+        m2iv = const.tile([P, D], F32, name="m2iv")
+        nc.gpsimd.tensor_tensor(out=m2iv[:], in0=mu[:], in1=miv32[:], op=ALU.mult)
         parts = const.tile([P, 3], F32, name="parts")
-        nc.vector.tensor_reduce(out=parts[:, 2:3], in_=m2iv[:], axis=AX.X, op=ALU.add)
+        nc.scalar.activation(
+            out=m2iv[:], in_=m2iv[:], func=ACT.Identity, accum_out=parts[:, 2:3]
+        )
+        junk = const.tile([P, 512], F32, name="junk")
         for h in range(2):
-            ld_ps = ps_w.tile([P, 512], F32, tag="w", name="ld_ps")
+            ld_ps = ps_t.tile([P, 512], F32, tag="yT", name="ld_ps")
             nc.tensor.matmul(
                 out=ld_ps[:], lhsT=center[:], rhs=lv[:, h * 512 : (h + 1) * 512], start=True, stop=True
             )
-            nc.vector.tensor_reduce(out=parts[:, h : h + 1], in_=ld_ps[:], axis=AX.X, op=ALU.add)
+            nc.scalar.activation(
+                out=junk[:], in_=ld_ps[:], func=ACT.Identity, accum_out=parts[:, h : h + 1]
+            )
         psum3 = const.tile([P, 1], F32, name="psum3")
         nc.vector.tensor_reduce(out=psum3[:], in_=parts[:], axis=AX.X, op=ALU.add)
         ybias = const.tile([P, 1], F32, name="ybias")
@@ -79,33 +115,8 @@ def tile_gmmoutlierdetector_t_kernel(tc, feats, means, log_vars, log_weights, ou
             out=ybias[:], in0=psum3[:], scalar=0.5, in1=lw[:], op0=ALU.mult, op1=ALU.subtract
         )
 
-        wb = const.tile([P, 2, G, PACK, P], BF16, name="wb")
-        nc.vector.tensor_copy(
-            out=wb[:, 0], in_=iv32[:].rearrange("c (g p t) -> c g t p", g=G, p=P, t=PACK)
-        )
-        nc.vector.tensor_scalar(
-            out=wb[:, 1],
-            in0=miv32[:].rearrange("c (g p t) -> c g t p", g=G, p=P, t=PACK),
-            scalar1=-2.0,
-            scalar2=None,
-            op0=ALU.mult,
-        )
-        wg = const.tile([P, 2 * G, P, PACK], BF16, name="wg", align_bytes=64)
-        for o in range(2):
-            for g in range(G):
-                wT = ps_w.tile([P, PACK, P], BF16, tag="w", name="wT")
-                for t in range(PACK):
-                    nc.tensor.transpose(wT[:, t, :], wb[:, o, g, t, :], ident_bf[:])
-                nc.vector.tensor_copy(
-                    out=wg[:, o * G + g], in_=wT[:].rearrange("p t c -> p c t")
-                )
-        wc = const.tile([P, 2 * G * P], U32, name="wc", align_bytes=64)
-        ws = const.tile([P, 2 * G * P], U8, name="ws", align_bytes=64)
-        nc.vector.quantize_mx(
-            out=wc[:].bitcast(FP8X4), scales=ws[:], in_=wg[:].rearrange("p a c t -> p (a c t)")
-        )
-
-        gs_all = const.tile([P, P * NCLS], F32, name="gs_all")
+        res = const.tile([P, P], F32, name="res")
+        s_ps = None
 
         for b in range(B):
             for h in range(HW // NLOAD):
@@ -155,32 +166,46 @@ def tile_gmmoutlierdetector_t_kernel(tc, feats, means, log_vars, log_weights, ou
                         nc.tensor.transpose(yT[:, j, :], y[:, j * P : (j + 1) * P], ident_f[:])
                     mn = work.tile([P, NT], F32, tag="mn", name="mn")
                     nc.vector.tensor_reduce(out=mn[:], in_=yT[:], axis=AX.X, op=ALU.min)
-                    e = work.tile([P, NT, P], F32, tag="e", name="e")
+                    e = work.tile([P, NCMP, NT, NCLS], F32, tag="e", name="e")
                     for j in range(NT):
                         nc.scalar.activation(
-                            out=e[:, j, :], in_=yT[:, j, :], func=ACT.Exp, bias=mn[:, j : j + 1], scale=-1.0
+                            out=e[:, :, j, :],
+                            in_=yT[:, j, :].rearrange("p (k m) -> p m k", m=NCMP),
+                            func=ACT.Exp,
+                            bias=mn[:, j : j + 1],
+                            scale=-1.0,
                         )
-                    nc.vector.tensor_reduce(
-                        out=gs_all[:, tile0 * NCLS : (tile0 + NT) * NCLS],
-                        in_=e[:].rearrange("p j (k m) -> p (j k) m", m=NCMP),
-                        axis=AX.X,
-                        op=ALU.add,
-                    )
+                    slot = tile0 % TB
+                    if slot == 0:
+                        s_ps = ps_s.tile([P, TB, NCLS], F32, tag="s", name="s_ps")
+                    for m in range(NCMP):
+                        nc.tensor.matmul(
+                            out=s_ps[:, slot : slot + NT, :].rearrange("p j k -> p (j k)"),
+                            lhsT=ident_f[:],
+                            rhs=e[:, m].rearrange("p j k -> p (j k)"),
+                            start=(m == 0),
+                            stop=(m == NCMP - 1),
+                        )
+                    if slot + NT == TB:
+                        t0 = tile0 + NT - TB
+                        top = work.tile([P, TB], F32, tag="top", name="top")
+                        nc.vector.tensor_reduce(out=top[:], in_=s_ps[:], axis=AX.X, op=ALU.max)
+                        tot = work.tile([P, TB], F32, tag="tot", name="tot")
+                        nc.vector.tensor_reduce(out=tot[:], in_=s_ps[:], axis=AX.X, op=ALU.add)
+                        rec = work.tile([P, TB], F32, tag="rec", name="rec")
+                        nc.vector.reciprocal(out=rec[:], in_=tot[:])
+                        share = work.tile([P, TB], F32, tag="share", name="share")
+                        nc.vector.tensor_tensor(out=share[:], in0=top[:], in1=rec[:], op=ALU.mult)
+                        nc.vector.tensor_scalar(
+                            out=res[:, t0 : t0 + TB],
+                            in0=share[:],
+                            scalar1=-1.0,
+                            scalar2=1.0,
+                            op0=ALU.mult,
+                            op1=ALU.add,
+                        )
 
-        gs_v = gs_all[:].rearrange("p (n k) -> p n k", k=NCLS)
-        top = const.tile([P, P], F32, name="top")
-        nc.vector.tensor_reduce(out=top[:], in_=gs_v, axis=AX.X, op=ALU.max)
-        tot = const.tile([P, P], F32, name="tot")
-        nc.vector.tensor_reduce(out=tot[:], in_=gs_v, axis=AX.X, op=ALU.add)
-        rec = const.tile([P, P], F32, name="rec")
-        nc.vector.reciprocal(out=rec[:], in_=tot[:])
-        share = const.tile([P, P], F32, name="share")
-        nc.vector.tensor_tensor(out=share[:], in0=top[:], in1=rec[:], op=ALU.mult)
-        res = const.tile([P, P], F32, name="res")
-        nc.vector.tensor_scalar(
-            out=res[:], in0=share[:], scalar1=-1.0, scalar2=1.0, op0=ALU.mult, op1=ALU.add
-        )
-        resT = ps_w.tile([P, P], F32, tag="w", name="resT")
+        resT = ps_t.tile([P, P], F32, tag="yT", name="resT")
         nc.tensor.transpose(resT[:], res[:], ident_f[:])
         res_sb = const.tile([P, P], F32, name="res_sb")
         nc.vector.tensor_copy(out=res_sb[:], in_=resT[:])

@@ -25,6 +25,10 @@ NT = NG // P
 NCLS = 16
 NCMP = 8
 TB = 32
+NGRP = B * HW // NG
+NUNIT = B * HW // NLOAD
+AHEAD = 4
+V_SQUARES = (NGRP - 1,)
 
 FLOPS = 2 * 2 * (B * HW) * D * P
 
@@ -33,13 +37,32 @@ def tile_gmmoutlierdetector_t_kernel(tc, feats, means, log_vars, log_weights, ou
     nc = tc.nc
     with ExitStack() as ctx:
         const = ctx.enter_context(tc.tile_pool(name="const", bufs=1))
-        rawp = ctx.enter_context(tc.tile_pool(name="rawp", bufs=4))
+        rawp = ctx.enter_context(tc.tile_pool(name="rawp", bufs=AHEAD))
         work = ctx.enter_context(tc.tile_pool(name="work", bufs=3))
-        ps_acc = ctx.enter_context(tc.psum_pool(name="ps_acc", bufs=2))
-        ps_t = ctx.enter_context(tc.psum_pool(name="ps_t", bufs=4))
+        ps_acc = ctx.enter_context(tc.psum_pool(name="ps_acc", bufs=3))
+        ps_t = ctx.enter_context(tc.psum_pool(name="ps_t", bufs=3))
         ps_s = ctx.enter_context(tc.psum_pool(name="ps_s", bufs=2))
+        ctx.enter_context(tc.manual_schedule())
 
         fv = feats.rearrange("b (g p t) h w -> b g p t (h w)", g=G, p=P, t=PACK)
+        st = {}
+
+        def load(u):
+            raw = rawp.tile([P, G, PACK, NLOAD], BF16, tag="raw", name="raw")
+            b, h = divmod(u, HW // NLOAD)
+            cuts = 2 if u == 0 else 1
+            w = NLOAD // cuts
+            for q in range(cuts):
+                for g in range(G):
+                    lo = h * NLOAD + q * w
+                    nc.sync.dma_start(
+                        out=raw[:, g, :, q * w : (q + 1) * w], in_=fv[b, g, :, :, lo : lo + w]
+                    )
+            st["raw", u] = raw
+
+        def raw_view(j, g):
+            n0 = (j % 2) * NG
+            return st["raw", j // 2][:, g, :, n0 : n0 + NG].rearrange("p t (c i) -> p c t i", i=4)
 
         lv = const.tile([P, D], BF16, name="lv")
         mu = const.tile([P, D], BF16, name="mu")
@@ -48,6 +71,8 @@ def tile_gmmoutlierdetector_t_kernel(tc, feats, means, log_vars, log_weights, ou
         nc.scalar.dma_start(out=mu[:], in_=means.rearrange("k m d -> (k m) d"))
         with nc.allow_non_contiguous_dma(reason="128 log weights, one to a partition"):
             nc.scalar.dma_start(out=lw[:], in_=log_weights.rearrange("k (m o) -> (k m) o", o=1))
+        for u in range(AHEAD):
+            load(u)
 
         ident_bf = const.tile([P, P], BF16, name="ident_bf")
         make_identity(nc, ident_bf[:])
@@ -57,153 +82,220 @@ def tile_gmmoutlierdetector_t_kernel(tc, feats, means, log_vars, log_weights, ou
         nc.vector.tensor_scalar(
             out=center[:], in0=ident_bf[:], scalar1=-1.0 / P, scalar2=None, op0=ALU.add
         )
+        perm = const.tile([P, P], F32, name="perm")
+        nc.vector.tensor_copy(
+            out=perm[:].rearrange("p (m k) -> p m k", m=NCMP),
+            in_=ident_f[:].rearrange("p (k m) -> p m k", m=NCMP),
+        )
 
         iv32 = const.tile([P, D], F32, name="iv32")
         nc.scalar.activation(out=iv32[:], in_=lv[:], func=ACT.Exp, scale=-1.0)
         miv32 = const.tile([P, D], F32, name="miv32")
         nc.gpsimd.tensor_tensor(out=miv32[:], in0=mu[:], in1=iv32[:], op=ALU.mult)
-
         wb = const.tile([P, 2, G, PACK, P], BF16, name="wb")
-        nc.gpsimd.tensor_scalar(
-            out=wb[:, 0],
-            in0=iv32[:].rearrange("c (g p t) -> c g t p", g=G, p=P, t=PACK),
-            scalar1=1.0,
-            scalar2=0.0,
-            op0=ALU.mult,
-            op1=ALU.add,
-        )
-        nc.gpsimd.tensor_scalar(
-            out=wb[:, 1],
-            in0=miv32[:].rearrange("c (g p t) -> c g t p", g=G, p=P, t=PACK),
-            scalar1=-2.0,
-            scalar2=0.0,
-            op0=ALU.mult,
-            op1=ALU.add,
-        )
-        wg = const.tile([P, 2 * G, P, PACK], BF16, name="wg", align_bytes=64)
-        for o in range(2):
-            for g in range(G):
-                wT = ps_t.tile([P, PACK, P], BF16, tag="yT", name="wT")
-                for t in range(PACK):
-                    nc.tensor.transpose(wT[:, t, :], wb[:, o, g, t, :], ident_bf[:])
-                nc.scalar.copy(out=wg[:, o * G + g], in_=wT[:].rearrange("p t c -> p c t"))
-        wc = const.tile([P, 2 * G * P], U32, name="wc", align_bytes=64)
-        ws = const.tile([P, 2 * G * P], U8, name="ws", align_bytes=64)
-        nc.vector.quantize_mx(
-            out=wc[:].bitcast(FP8X4), scales=ws[:], in_=wg[:].rearrange("p a c t -> p (a c t)")
-        )
-
+        for o, src, factor in ((1, miv32, -2.0), (0, iv32, 1.0)):
+            nc.gpsimd.tensor_scalar(
+                out=wb[:, o],
+                in0=src[:].rearrange("c (g p t) -> c g t p", g=G, p=P, t=PACK),
+                scalar1=factor,
+                scalar2=0.0,
+                op0=ALU.mult,
+                op1=ALU.add,
+            )
         m2iv = const.tile([P, D], F32, name="m2iv")
         nc.gpsimd.tensor_tensor(out=m2iv[:], in0=mu[:], in1=miv32[:], op=ALU.mult)
-        parts = const.tile([P, 3], F32, name="parts")
-        nc.scalar.activation(
-            out=m2iv[:], in_=m2iv[:], func=ACT.Identity, accum_out=parts[:, 2:3]
-        )
-        junk = const.tile([P, 512], F32, name="junk")
-        for h in range(2):
-            ld_ps = ps_t.tile([P, 512], F32, tag="yT", name="ld_ps")
+
+        wts = {}
+        for o in (1, 0):
+            wT = ps_t.tile([P, G, PACK, P], BF16, tag="yT", name="wT")
+            for g in range(G):
+                for t in range(PACK):
+                    nc.tensor.transpose(wT[:, g, t, :], wb[:, o, g, t, :], ident_bf[:])
+            wts[o] = wT
+        cst_ps = ps_acc.tile([P, 2, P], F32, tag="acc", name="cst_ps")
+        nblk = D // P
+        for i in range(nblk):
             nc.tensor.matmul(
-                out=ld_ps[:], lhsT=center[:], rhs=lv[:, h * 512 : (h + 1) * 512], start=True, stop=True
+                out=cst_ps[:, 0, :], lhsT=center[:], rhs=lv[:, i * P : (i + 1) * P],
+                start=(i == 0), stop=(i == nblk - 1),
             )
-            nc.scalar.activation(
-                out=junk[:], in_=ld_ps[:], func=ACT.Identity, accum_out=parts[:, h : h + 1]
+        for i in range(nblk):
+            nc.tensor.matmul(
+                out=cst_ps[:, 1, :], lhsT=ident_f[:], rhs=m2iv[:, i * P : (i + 1) * P],
+                start=(i == 0), stop=(i == nblk - 1),
             )
+        wg = const.tile([P, 2 * G, P, PACK], BF16, name="wg", align_bytes=64)
+        wc = const.tile([P, 2 * G * P], U32, name="wc", align_bytes=64)
+        ws = const.tile([P, 2 * G * P], U8, name="ws", align_bytes=64)
         psum3 = const.tile([P, 1], F32, name="psum3")
-        nc.vector.tensor_reduce(out=psum3[:], in_=parts[:], axis=AX.X, op=ALU.add)
         ybias = const.tile([P, 1], F32, name="ybias")
-        nc.vector.scalar_tensor_tensor(
-            out=ybias[:], in0=psum3[:], scalar=0.5, in1=lw[:], op0=ALU.mult, op1=ALU.subtract
-        )
-
         res = const.tile([P, P], F32, name="res")
-        s_ps = None
 
-        for b in range(B):
-            for h in range(HW // NLOAD):
-                raw = rawp.tile([P, G, PACK, NLOAD], BF16, tag="raw", name="raw")
-                for g in range(G):
-                    nc.sync.dma_start(
-                        out=raw[:, g], in_=fv[b, g, :, :, h * NLOAD : (h + 1) * NLOAD]
+        def weights_out_of_psum():
+            for o in (1, 0):
+                nc.scalar.copy(
+                    out=wg[:, o * G : (o + 1) * G], in_=wts[o][:].rearrange("p g t c -> p g c t")
+                )
+
+        def weights_quantise():
+            nc.vector.quantize_mx(
+                out=wc[:].bitcast(FP8X4), scales=ws[:], in_=wg[:].rearrange("p a c t -> p (a c t)")
+            )
+            nc.vector.tensor_reduce(out=psum3[:], in_=cst_ps[:], axis=AX.XY, op=ALU.add)
+            nc.vector.scalar_tensor_tensor(
+                out=ybias[:], in0=psum3[:], scalar=0.5, in1=lw[:], op0=ALU.mult, op1=ALU.subtract
+            )
+
+        def regroup(j):
+            xg = work.tile([P, G, NG, PACK], BF16, tag="xg", name="xg", align_bytes=64)
+            for g in range(G):
+                nc.vector.tensor_copy(
+                    out=xg[:, g].rearrange("p (c i) t -> p c t i", i=4), in_=raw_view(j, g)
+                )
+            st["xg", j] = xg
+
+        def square(j):
+            x2 = work.tile([P, G, NG, PACK], BF16, tag="x2", name="x2", align_bytes=64)
+            for g in range(G):
+                if g == G - 1 and j in V_SQUARES:
+                    xv = st["xg", j][:, g].rearrange("p n t -> p (n t)")
+                    nc.vector.tensor_tensor(
+                        out=x2[:, g].rearrange("p n t -> p (n t)"), in0=xv, in1=xv, op=ALU.mult
                     )
-                for q in range(NLOAD // NG):
-                    n0 = q * NG
-                    tile0 = (b * HW + h * NLOAD + n0) // P
-                    xg = work.tile([P, G, NG, PACK], BF16, tag="xg", name="xg", align_bytes=64)
-                    for g in range(G):
-                        nc.vector.tensor_copy(
-                            out=xg[:, g].rearrange("p (c i) t -> p c t i", i=4),
-                            in_=raw[:, g, :, n0 : n0 + NG].rearrange("p t (c i) -> p c t i", i=4),
-                        )
-                    xg_flat = xg[:].rearrange("p g n t -> p (g n t)")
-                    x2 = work.tile([P, G * NG * PACK], BF16, tag="x2", name="x2", align_bytes=64)
-                    nc.scalar.activation(out=x2[:], in_=xg_flat, func=ACT.Square)
-                    xc = work.tile([P, G * NG], U32, tag="xc", name="xc", align_bytes=64)
-                    xs = work.tile([P, G * NG], U8, tag="xs", name="xs", align_bytes=64)
-                    nc.vector.quantize_mx(out=xc[:].bitcast(FP8X4), scales=xs[:], in_=xg_flat)
-                    x2c = work.tile([P, G * NG], U32, tag="x2c", name="x2c", align_bytes=64)
-                    x2s = work.tile([P, G * NG], U8, tag="x2s", name="x2s", align_bytes=64)
-                    nc.vector.quantize_mx(out=x2c[:].bitcast(FP8X4), scales=x2s[:], in_=x2[:])
-
-                    acc = ps_acc.tile([P, NG], F32, tag="acc", name="acc")
-                    passes = [(1, g, xc, xs) for g in range(G)] + [(0, g, x2c, x2s) for g in range(G)]
-                    for idx, (o, g, codes, scales) in enumerate(passes):
-                        a = (o * G + g) * P
-                        nc.tensor.matmul_mx(
-                            out=acc[:],
-                            lhsT=wc[:, a : a + P].bitcast(FP8X4),
-                            lhsT_scale=ws[:, a : a + P],
-                            rhs=codes[:, g * NG : (g + 1) * NG].bitcast(FP8X4),
-                            rhs_scale=scales[:, g * NG : (g + 1) * NG],
-                            start=(idx == 0),
-                            stop=(idx == len(passes) - 1),
-                        )
-                    y = work.tile([P, NG], F32, tag="y", name="y")
+                else:
                     nc.scalar.activation(
-                        out=y[:], in_=acc[:], func=ACT.Identity, bias=ybias[:, 0:1], scale=0.5
+                        out=x2[:, g].rearrange("p (c i) t -> p c t i", i=4),
+                        in_=raw_view(j, g),
+                        func=ACT.Square,
                     )
-                    yT = ps_t.tile([P, NT, P], F32, tag="yT", name="yT")
-                    for j in range(NT):
-                        nc.tensor.transpose(yT[:, j, :], y[:, j * P : (j + 1) * P], ident_f[:])
-                    mn = work.tile([P, NT], F32, tag="mn", name="mn")
-                    nc.vector.tensor_reduce(out=mn[:], in_=yT[:], axis=AX.X, op=ALU.min)
-                    e = work.tile([P, NCMP, NT, NCLS], F32, tag="e", name="e")
-                    for j in range(NT):
-                        nc.scalar.activation(
-                            out=e[:, :, j, :],
-                            in_=yT[:, j, :].rearrange("p (k m) -> p m k", m=NCMP),
-                            func=ACT.Exp,
-                            bias=mn[:, j : j + 1],
-                            scale=-1.0,
-                        )
-                    slot = tile0 % TB
-                    if slot == 0:
-                        s_ps = ps_s.tile([P, TB, NCLS], F32, tag="s", name="s_ps")
-                    for m in range(NCMP):
-                        nc.tensor.matmul(
-                            out=s_ps[:, slot : slot + NT, :].rearrange("p j k -> p (j k)"),
-                            lhsT=ident_f[:],
-                            rhs=e[:, m].rearrange("p j k -> p (j k)"),
-                            start=(m == 0),
-                            stop=(m == NCMP - 1),
-                        )
-                    if slot + NT == TB:
-                        t0 = tile0 + NT - TB
-                        top = work.tile([P, TB], F32, tag="top", name="top")
-                        nc.vector.tensor_reduce(out=top[:], in_=s_ps[:], axis=AX.X, op=ALU.max)
-                        tot = work.tile([P, TB], F32, tag="tot", name="tot")
-                        nc.vector.tensor_reduce(out=tot[:], in_=s_ps[:], axis=AX.X, op=ALU.add)
-                        rec = work.tile([P, TB], F32, tag="rec", name="rec")
-                        nc.vector.reciprocal(out=rec[:], in_=tot[:])
-                        share = work.tile([P, TB], F32, tag="share", name="share")
-                        nc.vector.tensor_tensor(out=share[:], in0=top[:], in1=rec[:], op=ALU.mult)
-                        nc.vector.tensor_scalar(
-                            out=res[:, t0 : t0 + TB],
-                            in0=share[:],
-                            scalar1=-1.0,
-                            scalar2=1.0,
-                            op0=ALU.mult,
-                            op1=ALU.add,
-                        )
+            st["x2", j] = x2
+
+        def quantise(j, what):
+            codes = work.tile([P, G * NG], U32, tag=what + "c", name="codes", align_bytes=64)
+            scales = work.tile([P, G * NG], U8, tag=what + "s", name="scales", align_bytes=64)
+            nc.vector.quantize_mx(
+                out=codes[:].bitcast(FP8X4),
+                scales=scales[:],
+                in_=st[what, j][:].rearrange("p g n t -> p (g n t)"),
+            )
+            st[what + "q", j] = (codes, scales)
+
+        def products(j):
+            acc = ps_acc.tile([P, NG], F32, tag="acc", name="acc")
+            passes = [(1, g, "xgq") for g in range(G)] + [(0, g, "x2q") for g in range(G)]
+            for idx, (o, g, what) in enumerate(passes):
+                codes, scales = st[what, j]
+                a = (o * G + g) * P
+                nc.tensor.matmul_mx(
+                    out=acc[:],
+                    lhsT=wc[:, a : a + P].bitcast(FP8X4),
+                    lhsT_scale=ws[:, a : a + P],
+                    rhs=codes[:, g * NG : (g + 1) * NG].bitcast(FP8X4),
+                    rhs_scale=scales[:, g * NG : (g + 1) * NG],
+                    start=(idx == 0),
+                    stop=(idx == len(passes) - 1),
+                )
+            st["acc", j] = acc
+
+        def leave_psum(j):
+            y = work.tile([P, NG], F32, tag="y", name="y")
+            nc.scalar.activation(
+                out=y[:], in_=st["acc", j][:], func=ACT.Identity, bias=ybias[:, 0:1], scale=0.5
+            )
+            st["y", j] = y
+
+        def turn(j):
+            yT = ps_t.tile([P, NT, P], F32, tag="yT", name="yT")
+            for i in range(NT):
+                nc.tensor.transpose(yT[:, i, :], st["y", j][:, i * P : (i + 1) * P], perm[:])
+            st["yT", j] = yT
+
+        def smallest(j):
+            mn = work.tile([P, NT], F32, tag="mn", name="mn")
+            nc.vector.tensor_reduce(out=mn[:], in_=st["yT", j][:], axis=AX.X, op=ALU.min)
+            st["mn", j] = mn
+
+        def exponent(j):
+            e = work.tile([P, NCMP, NT, NCLS], F32, tag="e", name="e")
+            for i in range(NT):
+                nc.scalar.activation(
+                    out=e[:, :, i, :],
+                    in_=st["yT", j][:, i, :].rearrange("p (m k) -> p m k", m=NCMP),
+                    func=ACT.Exp,
+                    bias=st["mn", j][:, i : i + 1],
+                    scale=-1.0,
+                )
+            st["e", j] = e
+
+        def class_sums(j):
+            slot = (j * NT) % TB
+            if slot == 0:
+                st["s", j * NT // TB] = ps_s.tile([P, TB, NCLS], F32, tag="s", name="s_ps")
+            s_ps = st["s", j * NT // TB]
+            for m in range(NCMP):
+                nc.tensor.matmul(
+                    out=s_ps[:, slot : slot + NT, :].rearrange("p i k -> p (i k)"),
+                    lhsT=ident_f[:],
+                    rhs=st["e", j][:, m].rearrange("p i k -> p (i k)"),
+                    start=(m == 0),
+                    stop=(m == NCMP - 1),
+                )
+
+        def finish(t_lo, t_hi):
+            n = t_hi - t_lo
+            sv = st["s", t_lo // TB][:, t_lo % TB : t_lo % TB + n, :]
+            top = work.tile([P, TB], F32, tag="top", name="top")
+            nc.vector.tensor_reduce(out=top[:, :n], in_=sv, axis=AX.X, op=ALU.max)
+            tot = work.tile([P, TB], F32, tag="tot", name="tot")
+            nc.vector.tensor_reduce(out=tot[:, :n], in_=sv, axis=AX.X, op=ALU.add)
+            rec = work.tile([P, TB], F32, tag="rec", name="rec")
+            nc.vector.reciprocal(out=rec[:, :n], in_=tot[:, :n])
+            share = work.tile([P, TB], F32, tag="share", name="share")
+            nc.vector.tensor_tensor(out=share[:, :n], in0=top[:, :n], in1=rec[:, :n], op=ALU.mult)
+            nc.vector.tensor_scalar(
+                out=res[:, t_lo:t_hi], in0=share[:, :n], scalar1=-1.0, scalar2=1.0,
+                op0=ALU.mult, op1=ALU.add,
+            )
+
+        waiting = []
+        due = []
+        for j in range(NGRP + 4):
+            if j < NGRP:
+                regroup(j)
+                square(j)
+                if j % 2 == 1 and j // 2 + AHEAD < NUNIT:
+                    load(j // 2 + AHEAD)
+            if j == 1:
+                weights_out_of_psum()
+            if 0 <= j - 1 < NGRP:
+                quantise(j - 1, "x2")
+                waiting.append(j - 1)
+            if j == 2:
+                weights_quantise()
+            if j >= 2:
+                for i in waiting:
+                    products(i)
+                waiting = []
+            if j < NGRP:
+                quantise(j, "xg")
+            if 0 <= j - 3 < NGRP:
+                smallest(j - 3)
+            for t_lo, t_hi in due:
+                finish(t_lo, t_hi)
+            due = []
+            if 0 <= j - 2 < NGRP:
+                leave_psum(j - 2)
+                turn(j - 2)
+            if 0 <= j - 3 < NGRP:
+                exponent(j - 3)
+                class_sums(j - 3)
+                done = (j - 3 + 1) * NT
+                if done % TB == 0 and done < P:
+                    due.append((done - TB, done))
+                if done == P - NT:
+                    due.append((P - TB, done))
+                if done == P:
+                    finish(P - NT, P)
 
         resT = ps_t.tile([P, P], F32, tag="yT", name="resT")
         nc.tensor.transpose(resT[:], res[:], ident_f[:])

@@ -29,6 +29,8 @@ NGRP = B * HW // NG
 NUNIT = B * HW // NLOAD
 AHEAD = 4
 V_SQUARES = (NGRP - 1,)
+BATCHES = ((0, 8), (8, 8), (16, 8), (24, 4), (28, 2))
+V_SUMS = (30, 31)
 
 FLOPS = 2 * 2 * (B * HW) * D * P
 
@@ -39,6 +41,7 @@ def tile_gmmoutlierdetector_t_kernel(tc, feats, means, log_vars, log_weights, ou
         const = ctx.enter_context(tc.tile_pool(name="const", bufs=1))
         rawp = ctx.enter_context(tc.tile_pool(name="rawp", bufs=AHEAD))
         work = ctx.enter_context(tc.tile_pool(name="work", bufs=3))
+        ebp = ctx.enter_context(tc.tile_pool(name="ebp", bufs=2))
         ps_acc = ctx.enter_context(tc.psum_pool(name="ps_acc", bufs=3))
         ps_t = ctx.enter_context(tc.psum_pool(name="ps_t", bufs=3))
         ps_s = ctx.enter_context(tc.psum_pool(name="ps_s", bufs=2))
@@ -207,7 +210,9 @@ def tile_gmmoutlierdetector_t_kernel(tc, feats, means, log_vars, log_weights, ou
         def turn(j):
             yT = ps_t.tile([P, NT, P], F32, tag="yT", name="yT")
             for i in range(NT):
-                nc.tensor.transpose(yT[:, i, :], st["y", j][:, i * P : (i + 1) * P], perm[:])
+                nc.tensor.transpose(
+                    yT[:, i, :], st["y", j][:, i * P : (i + 1) * P], ident_f[:] if j in V_SUMS else perm[:]
+                )
             st["yT", j] = yT
 
         def smallest(j):
@@ -215,35 +220,55 @@ def tile_gmmoutlierdetector_t_kernel(tc, feats, means, log_vars, log_weights, ou
             nc.vector.tensor_reduce(out=mn[:], in_=st["yT", j][:], axis=AX.X, op=ALU.min)
             st["mn", j] = mn
 
+        def batch_of(j):
+            for first, count in BATCHES:
+                if first <= j < first + count:
+                    return first, count
+            return None
+
         def exponent(j):
-            e = work.tile([P, NCMP, NT, NCLS], F32, tag="e", name="e")
+            if j in V_SUMS:
+                e = work.tile([P, NT, P], F32, tag="e", name="e")
+                outs = [e[:, i, :] for i in range(NT)]
+                ins = [st["yT", j][:, i, :] for i in range(NT)]
+                st["e", j] = e
+            else:
+                first, count = batch_of(j)
+                if j == first:
+                    st["eb", first] = ebp.tile([P, NCMP, count * NT, NCLS], F32, tag="eb", name="eb")
+                eb = st["eb", first]
+                outs = [eb[:, :, (j - first) * NT + i, :] for i in range(NT)]
+                ins = [
+                    st["yT", j][:, i, :].rearrange("p (m k) -> p m k", m=NCMP) for i in range(NT)
+                ]
             for i in range(NT):
                 nc.scalar.activation(
-                    out=e[:, :, i, :],
-                    in_=st["yT", j][:, i, :].rearrange("p (m k) -> p m k", m=NCMP),
-                    func=ACT.Exp,
-                    bias=st["mn", j][:, i : i + 1],
-                    scale=-1.0,
-                )
-            st["e", j] = e
-
-        def class_sums(j):
-            slot = (j * NT) % TB
-            if slot == 0:
-                st["s", j * NT // TB] = ps_s.tile([P, TB, NCLS], F32, tag="s", name="s_ps")
-            s_ps = st["s", j * NT // TB]
-            for m in range(NCMP):
-                nc.tensor.matmul(
-                    out=s_ps[:, slot : slot + NT, :].rearrange("p i k -> p (i k)"),
-                    lhsT=ident_f[:],
-                    rhs=st["e", j][:, m].rearrange("p i k -> p (i k)"),
-                    start=(m == 0),
-                    stop=(m == NCMP - 1),
+                    out=outs[i], in_=ins[i], func=ACT.Exp, bias=st["mn", j][:, i : i + 1], scale=-1.0
                 )
 
-        def finish(t_lo, t_hi):
+        def plane(first, count, m):
+            if m == 0:
+                st["s", first] = ps_s.tile([P, TB, NCLS], F32, tag="s", name="s_ps")
+            nc.tensor.matmul(
+                out=st["s", first][:, : count * NT, :].rearrange("p i k -> p (i k)"),
+                lhsT=ident_f[:],
+                rhs=st["eb", first][:, m].rearrange("p i k -> p (i k)"),
+                start=(m == 0),
+                stop=(m == NCMP - 1),
+            )
+
+        def vector_sums(j):
+            gs = work.tile([P, NT, NCLS], F32, tag="gs", name="gs")
+            nc.vector.tensor_reduce(
+                out=gs[:],
+                in_=st["e", j][:].rearrange("p i (k m) -> p i k m", m=NCMP),
+                axis=AX.X,
+                op=ALU.add,
+            )
+            return gs
+
+        def finish(sv, t_lo, t_hi):
             n = t_hi - t_lo
-            sv = st["s", t_lo // TB][:, t_lo % TB : t_lo % TB + n, :]
             top = work.tile([P, TB], F32, tag="top", name="top")
             nc.vector.tensor_reduce(out=top[:, :n], in_=sv, axis=AX.X, op=ALU.max)
             tot = work.tile([P, TB], F32, tag="tot", name="tot")
@@ -259,6 +284,8 @@ def tile_gmmoutlierdetector_t_kernel(tc, feats, means, log_vars, log_weights, ou
 
         waiting = []
         due = []
+        planes = []
+        late = []
         for j in range(NGRP + 4):
             if j < NGRP:
                 regroup(j)
@@ -280,22 +307,30 @@ def tile_gmmoutlierdetector_t_kernel(tc, feats, means, log_vars, log_weights, ou
                 quantise(j, "xg")
             if 0 <= j - 3 < NGRP:
                 smallest(j - 3)
-            for t_lo, t_hi in due:
-                finish(t_lo, t_hi)
+            for first, count in due:
+                finish(st["s", first][:, : count * NT, :], first * NT, (first + count) * NT)
             due = []
+            for i in late:
+                finish(vector_sums(i)[:], i * NT, (i + 1) * NT)
+            late = []
             if 0 <= j - 2 < NGRP:
                 leave_psum(j - 2)
                 turn(j - 2)
             if 0 <= j - 3 < NGRP:
                 exponent(j - 3)
-                class_sums(j - 3)
-                done = (j - 3 + 1) * NT
-                if done % TB == 0 and done < P:
-                    due.append((done - TB, done))
-                if done == P - NT:
-                    due.append((P - TB, done))
-                if done == P:
-                    finish(P - NT, P)
+                if j - 3 in V_SUMS:
+                    late.append(j - 3)
+                else:
+                    first, count = batch_of(j - 3)
+                    if j - 3 == first + count - 1:
+                        planes.extend([(first, count, m) for m in range(NCMP)])
+            for i in range(2 if planes and planes[0][1] == 8 else 4):
+                if planes:
+                    first, count, m = planes[0]
+                    planes = planes[1:]
+                    plane(first, count, m)
+                    if m == NCMP - 1:
+                        due.append((first, count))
 
         resT = ps_t.tile([P, P], F32, tag="yT", name="resT")
         nc.tensor.transpose(resT[:], res[:], ident_f[:])

@@ -28,7 +28,8 @@ TB = 32
 NGRP = B * HW // NG
 NUNIT = B * HW // NLOAD
 AHEAD = 4
-V_SQUARES = (NGRP - 1,)
+V_SHARE = 96
+V_SHARE_LAST = NG
 BATCHES = ((0, 8), (8, 8), (16, 8), (24, 4), (28, 2))
 V_SUMS = (30, 31)
 
@@ -157,21 +158,30 @@ def tile_gmmoutlierdetector_t_kernel(tc, feats, means, log_vars, log_weights, ou
                 )
             st["xg", j] = xg
 
-        def square(j):
+        def v_share(j):
+            return V_SHARE_LAST if j == NGRP - 1 else V_SHARE
+
+        def square_scalar(j):
             x2 = work.tile([P, G, NG, PACK], BF16, tag="x2", name="x2", align_bytes=64)
             for g in range(G):
-                if g == G - 1 and j in V_SQUARES:
-                    xv = st["xg", j][:, g].rearrange("p n t -> p (n t)")
-                    nc.vector.tensor_tensor(
-                        out=x2[:, g].rearrange("p n t -> p (n t)"), in0=xv, in1=xv, op=ALU.mult
-                    )
-                else:
+                n = NG - v_share(j) if g == G - 1 else NG
+                if n > 0:
                     nc.scalar.activation(
-                        out=x2[:, g].rearrange("p (c i) t -> p c t i", i=4),
-                        in_=raw_view(j, g),
+                        out=x2[:, g, :n, :].rearrange("p (c i) t -> p c t i", i=4),
+                        in_=raw_view(j, g)[:, : n // 4],
                         func=ACT.Square,
                     )
             st["x2", j] = x2
+
+        def square_vector(j):
+            lo = NG - v_share(j)
+            xv = st["xg", j][:, G - 1, lo:, :].rearrange("p n t -> p (n t)")
+            nc.vector.tensor_tensor(
+                out=st["x2", j][:, G - 1, lo:, :].rearrange("p n t -> p (n t)"),
+                in0=xv,
+                in1=xv,
+                op=ALU.mult,
+            )
 
         def quantise(j, what):
             codes = work.tile([P, G * NG], U32, tag=what + "c", name="codes", align_bytes=64)
@@ -289,7 +299,7 @@ def tile_gmmoutlierdetector_t_kernel(tc, feats, means, log_vars, log_weights, ou
         for j in range(NGRP + 4):
             if j < NGRP:
                 regroup(j)
-                square(j)
+                square_scalar(j)
                 if j % 2 == 1 and j // 2 + AHEAD < NUNIT:
                     load(j // 2 + AHEAD)
             if j == 1:
@@ -297,6 +307,8 @@ def tile_gmmoutlierdetector_t_kernel(tc, feats, means, log_vars, log_weights, ou
             if 0 <= j - 1 < NGRP:
                 quantise(j - 1, "x2")
                 waiting.append(j - 1)
+            if j < NGRP:
+                square_vector(j)
             if j == 2:
                 weights_quantise()
             if j >= 2:

@@ -28,9 +28,9 @@ TB = 32
 NGRP = B * HW // NG
 NUNIT = B * HW // NLOAD
 AHEAD = 4
-V_SHARE = 96
+V_SHARE = 64
 V_SHARE_LAST = NG
-BATCHES = ((0, 8), (8, 8), (16, 8), (24, 4), (28, 2))
+PAIR = 2
 V_SUMS = (30, 31)
 
 FLOPS = 2 * 2 * (B * HW) * D * P
@@ -42,10 +42,10 @@ def tile_gmmoutlierdetector_t_kernel(tc, feats, means, log_vars, log_weights, ou
         const = ctx.enter_context(tc.tile_pool(name="const", bufs=1))
         rawp = ctx.enter_context(tc.tile_pool(name="rawp", bufs=AHEAD))
         work = ctx.enter_context(tc.tile_pool(name="work", bufs=3))
-        ebp = ctx.enter_context(tc.tile_pool(name="ebp", bufs=2))
-        ps_acc = ctx.enter_context(tc.psum_pool(name="ps_acc", bufs=3))
+        ps_acc = ctx.enter_context(tc.psum_pool(name="ps_acc", bufs=2))
         ps_t = ctx.enter_context(tc.psum_pool(name="ps_t", bufs=3))
         ps_s = ctx.enter_context(tc.psum_pool(name="ps_s", bufs=2))
+        ps_u = ctx.enter_context(tc.psum_pool(name="ps_u", bufs=1))
         ctx.enter_context(tc.manual_schedule())
 
         fv = feats.rearrange("b (g p t) h w -> b g p t (h w)", g=G, p=P, t=PACK)
@@ -116,7 +116,7 @@ def tile_gmmoutlierdetector_t_kernel(tc, feats, means, log_vars, log_weights, ou
                 for t in range(PACK):
                     nc.tensor.transpose(wT[:, g, t, :], wb[:, o, g, t, :], ident_bf[:])
             wts[o] = wT
-        cst_ps = ps_acc.tile([P, 2, P], F32, tag="acc", name="cst_ps")
+        cst_ps = ps_u.tile([P, 2, P], F32, tag="u", name="cst_ps")
         nblk = D // P
         for i in range(nblk):
             nc.tensor.matmul(
@@ -230,12 +230,6 @@ def tile_gmmoutlierdetector_t_kernel(tc, feats, means, log_vars, log_weights, ou
             nc.vector.tensor_reduce(out=mn[:], in_=st["yT", j][:], axis=AX.X, op=ALU.min)
             st["mn", j] = mn
 
-        def batch_of(j):
-            for first, count in BATCHES:
-                if first <= j < first + count:
-                    return first, count
-            return None
-
         def exponent(j):
             if j in V_SUMS:
                 e = work.tile([P, NT, P], F32, tag="e", name="e")
@@ -243,11 +237,12 @@ def tile_gmmoutlierdetector_t_kernel(tc, feats, means, log_vars, log_weights, ou
                 ins = [st["yT", j][:, i, :] for i in range(NT)]
                 st["e", j] = e
             else:
-                first, count = batch_of(j)
-                if j == first:
-                    st["eb", first] = ebp.tile([P, NCMP, count * NT, NCLS], F32, tag="eb", name="eb")
-                eb = st["eb", first]
-                outs = [eb[:, :, (j - first) * NT + i, :] for i in range(NT)]
+                if j % PAIR == 0:
+                    st["eb", j // PAIR] = work.tile(
+                        [P, NCMP, PAIR * NT, NCLS], F32, tag="eb", name="eb"
+                    )
+                eb = st["eb", j // PAIR]
+                outs = [eb[:, :, (j % PAIR) * NT + i, :] for i in range(NT)]
                 ins = [
                     st["yT", j][:, i, :].rearrange("p (m k) -> p m k", m=NCMP) for i in range(NT)
                 ]
@@ -256,15 +251,30 @@ def tile_gmmoutlierdetector_t_kernel(tc, feats, means, log_vars, log_weights, ou
                     out=outs[i], in_=ins[i], func=ACT.Exp, bias=st["mn", j][:, i : i + 1], scale=-1.0
                 )
 
-        def plane(first, count, m):
-            if m == 0:
-                st["s", first] = ps_s.tile([P, TB, NCLS], F32, tag="s", name="s_ps")
-            nc.tensor.matmul(
-                out=st["s", first][:, : count * NT, :].rearrange("p i k -> p (i k)"),
-                lhsT=ident_f[:],
-                rhs=st["eb", first][:, m].rearrange("p i k -> p (i k)"),
-                start=(m == 0),
-                stop=(m == NCMP - 1),
+        def pair_sums(q):
+            sT = ps_u.tile([P, P], F32, tag="u", name="sT")
+            for m in range(NCMP):
+                nc.tensor.matmul(
+                    out=sT[:],
+                    lhsT=st["eb", q][:, m].rearrange("p i k -> p (i k)"),
+                    rhs=ident_f[:],
+                    start=(m == 0),
+                    stop=(m == NCMP - 1),
+                    is_transpose=True,
+                )
+            st["sT", q] = sT
+
+        def pair_back(q):
+            sT_sb = work.tile([P, P], F32, tag="sT_sb", name="sT_sb")
+            nc.vector.tensor_copy(out=sT_sb[:], in_=st["sT", q][:])
+            t_lo = q * PAIR * NT
+            if t_lo % TB == 0:
+                st["s", t_lo // TB] = ps_s.tile([P, TB, NCLS], F32, tag="s", name="s_ps")
+            slot = t_lo % TB
+            nc.tensor.transpose(
+                st["s", t_lo // TB][:, slot : slot + PAIR * NT, :].rearrange("p i k -> p (i k)"),
+                sT_sb[:],
+                ident_f[:],
             )
 
         def vector_sums(j):
@@ -292,9 +302,10 @@ def tile_gmmoutlierdetector_t_kernel(tc, feats, means, log_vars, log_weights, ou
                 op0=ALU.mult, op1=ALU.add,
             )
 
+        n_pairs = min(V_SUMS) // PAIR
         waiting = []
+        summed = []
         due = []
-        planes = []
         late = []
         for j in range(NGRP + 4):
             if j < NGRP:
@@ -319,8 +330,8 @@ def tile_gmmoutlierdetector_t_kernel(tc, feats, means, log_vars, log_weights, ou
                 quantise(j, "xg")
             if 0 <= j - 3 < NGRP:
                 smallest(j - 3)
-            for first, count in due:
-                finish(st["s", first][:, : count * NT, :], first * NT, (first + count) * NT)
+            for t_lo, t_hi in due:
+                finish(st["s", t_lo // TB][:, : t_hi - t_lo, :], t_lo, t_hi)
             due = []
             for i in late:
                 finish(vector_sums(i)[:], i * NT, (i + 1) * NT)
@@ -328,21 +339,19 @@ def tile_gmmoutlierdetector_t_kernel(tc, feats, means, log_vars, log_weights, ou
             if 0 <= j - 2 < NGRP:
                 leave_psum(j - 2)
                 turn(j - 2)
+            for q in summed:
+                pair_back(q)
+                t_hi = (q + 1) * PAIR * NT
+                if t_hi % TB == 0 or q == n_pairs - 1:
+                    due.append((t_hi - 1 - (t_hi - 1) % TB, t_hi))
+            summed = []
             if 0 <= j - 3 < NGRP:
                 exponent(j - 3)
                 if j - 3 in V_SUMS:
                     late.append(j - 3)
-                else:
-                    first, count = batch_of(j - 3)
-                    if j - 3 == first + count - 1:
-                        planes.extend([(first, count, m) for m in range(NCMP)])
-            for i in range(2 if planes and planes[0][1] == 8 else 4):
-                if planes:
-                    first, count, m = planes[0]
-                    planes = planes[1:]
-                    plane(first, count, m)
-                    if m == NCMP - 1:
-                        due.append((first, count))
+                elif (j - 3) % PAIR == PAIR - 1:
+                    pair_sums((j - 3) // PAIR)
+                    summed.append((j - 3) // PAIR)
 
         resT = ps_t.tile([P, P], F32, tag="yT", name="resT")
         nc.tensor.transpose(resT[:], res[:], ident_f[:])

@@ -19,7 +19,7 @@ B = 8
 D = 1024
 HW = 2048
 G = D // K_PASS
-NLOAD = 1024
+NLOAD = HW
 NG = 512
 NT = NG // P
 NCLS = 16
@@ -27,7 +27,8 @@ NCMP = 8
 TB = 32
 NGRP = B * HW // NG
 NUNIT = B * HW // NLOAD
-AHEAD = 4
+AHEAD = 2
+UG = NLOAD // NG
 V_SHARE = 64
 V_SHARE_LAST = NG
 PAIR = 2
@@ -53,20 +54,15 @@ def tile_gmmoutlierdetector_t_kernel(tc, feats, means, log_vars, log_weights, ou
 
         def load(u):
             raw = rawp.tile([P, G, PACK, NLOAD], BF16, tag="raw", name="raw")
-            b, h = divmod(u, HW // NLOAD)
-            cuts = 2 if u == 0 else 1
-            w = NLOAD // cuts
-            for q in range(cuts):
+            cuts = (0, NG, NLOAD) if u == 0 else (0, NLOAD)
+            for lo, hi in zip(cuts[:-1], cuts[1:]):
                 for g in range(G):
-                    lo = h * NLOAD + q * w
-                    nc.sync.dma_start(
-                        out=raw[:, g, :, q * w : (q + 1) * w], in_=fv[b, g, :, :, lo : lo + w]
-                    )
+                    nc.sync.dma_start(out=raw[:, g, :, lo:hi], in_=fv[u, g, :, :, lo:hi])
             st["raw", u] = raw
 
         def raw_view(j, g):
-            n0 = (j % 2) * NG
-            return st["raw", j // 2][:, g, :, n0 : n0 + NG].rearrange("p t (c i) -> p c t i", i=4)
+            n0 = (j % UG) * NG
+            return st["raw", j // UG][:, g, :, n0 : n0 + NG].rearrange("p t (c i) -> p c t i", i=4)
 
         lv = const.tile([P, D], BF16, name="lv")
         mu = const.tile([P, D], BF16, name="mu")
@@ -311,8 +307,8 @@ def tile_gmmoutlierdetector_t_kernel(tc, feats, means, log_vars, log_weights, ou
             if j < NGRP:
                 regroup(j)
                 square_scalar(j)
-                if j % 2 == 1 and j // 2 + AHEAD < NUNIT:
-                    load(j // 2 + AHEAD)
+                if j % UG == UG - 1 and j // UG + AHEAD < NUNIT:
+                    load(j // UG + AHEAD)
             if j == 1:
                 weights_out_of_psum()
             if 0 <= j - 1 < NGRP:

@@ -14,34 +14,30 @@ AX = mybir.AxisListType
 
 P = 128
 PACK = 4
-K_PASS = P * PACK
-B = 8
-D = 1024
-HW = 2048
-G = D // K_PASS
-NLOAD = HW
+IMAGES = 8
+CHANNELS = 1024
+PIXELS = 2048
+G = CHANNELS // (P * PACK)
 NG = 512
 NT = NG // P
+UG = PIXELS // NG
+NGRP = IMAGES * UG
 NCLS = 16
 NCMP = 8
-TB = 32
-NGRP = B * HW // NG
-NUNIT = B * HW // NLOAD
-AHEAD = 2
-UG = NLOAD // NG
-V_SHARE = 64
-V_SHARE_LAST = NG
 PAIR = 2
-V_SUMS = (30, 31)
+TB = 32
+RESIDENT = 2
+V_SHARE = 64
+V_SUMS = (NGRP - 2, NGRP - 1)
 
-FLOPS = 2 * 2 * (B * HW) * D * P
+FLOPS = 2 * 2 * (IMAGES * PIXELS) * CHANNELS * P
 
 
 def tile_gmmoutlierdetector_t_kernel(tc, feats, means, log_vars, log_weights, out):
     nc = tc.nc
     with ExitStack() as ctx:
         const = ctx.enter_context(tc.tile_pool(name="const", bufs=1))
-        rawp = ctx.enter_context(tc.tile_pool(name="rawp", bufs=AHEAD))
+        rawp = ctx.enter_context(tc.tile_pool(name="rawp", bufs=RESIDENT))
         work = ctx.enter_context(tc.tile_pool(name="work", bufs=3))
         ps_acc = ctx.enter_context(tc.psum_pool(name="ps_acc", bufs=2))
         ps_t = ctx.enter_context(tc.psum_pool(name="ps_t", bufs=3))
@@ -53,25 +49,28 @@ def tile_gmmoutlierdetector_t_kernel(tc, feats, means, log_vars, log_weights, ou
         st = {}
 
         def load(u):
-            raw = rawp.tile([P, G, PACK, NLOAD], BF16, tag="raw", name="raw")
-            cuts = (0, NG, NLOAD) if u == 0 else (0, NLOAD)
-            for lo, hi in zip(cuts[:-1], cuts[1:]):
+            raw = rawp.tile([P, G, PACK, PIXELS], BF16, tag="raw", name="raw")
+            if u == 0:
+                cuts = (0, NG, 2 * NG, PIXELS)
+                for lo, hi in zip(cuts[:-1], cuts[1:]):
+                    for g in range(G):
+                        for t in range(PACK):
+                            nc.sync.dma_start(out=raw[:, g, t, lo:hi], in_=fv[u, g, :, t, lo:hi])
+            else:
                 for g in range(G):
-                    nc.sync.dma_start(out=raw[:, g, :, lo:hi], in_=fv[u, g, :, :, lo:hi])
+                    nc.sync.dma_start(out=raw[:, g], in_=fv[u, g])
             st["raw", u] = raw
 
         def raw_view(j, g):
             n0 = (j % UG) * NG
             return st["raw", j // UG][:, g, :, n0 : n0 + NG].rearrange("p t (c i) -> p c t i", i=4)
 
-        lv = const.tile([P, D], BF16, name="lv")
-        mu = const.tile([P, D], BF16, name="mu")
+        lv = const.tile([P, CHANNELS], BF16, name="lv")
+        mu = const.tile([P, CHANNELS], BF16, name="mu")
         lw = const.tile([P, 1], BF16, name="lw")
         nc.scalar.dma_start(out=lv[:], in_=log_vars.rearrange("k m d -> (k m) d"))
         nc.scalar.dma_start(out=mu[:], in_=means.rearrange("k m d -> (k m) d"))
-        with nc.allow_non_contiguous_dma(reason="128 log weights, one to a partition"):
-            nc.scalar.dma_start(out=lw[:], in_=log_weights.rearrange("k (m o) -> (k m) o", o=1))
-        for u in range(AHEAD):
+        for u in range(RESIDENT):
             load(u)
 
         ident_bf = const.tile([P, P], BF16, name="ident_bf")
@@ -88,9 +87,11 @@ def tile_gmmoutlierdetector_t_kernel(tc, feats, means, log_vars, log_weights, ou
             in_=ident_f[:].rearrange("p (k m) -> p m k", m=NCMP),
         )
 
-        iv32 = const.tile([P, D], F32, name="iv32")
+        iv32 = const.tile([P, CHANNELS], F32, name="iv32")
         nc.scalar.activation(out=iv32[:], in_=lv[:], func=ACT.Exp, scale=-1.0)
-        miv32 = const.tile([P, D], F32, name="miv32")
+        with nc.allow_non_contiguous_dma(reason="128 log weights, one to a partition"):
+            nc.scalar.dma_start(out=lw[:], in_=log_weights.rearrange("k (m o) -> (k m) o", o=1))
+        miv32 = const.tile([P, CHANNELS], F32, name="miv32")
         nc.gpsimd.tensor_tensor(out=miv32[:], in0=mu[:], in1=iv32[:], op=ALU.mult)
         wb = const.tile([P, 2, G, PACK, P], BF16, name="wb")
         for o, src, factor in ((1, miv32, -2.0), (0, iv32, 1.0)):
@@ -102,7 +103,7 @@ def tile_gmmoutlierdetector_t_kernel(tc, feats, means, log_vars, log_weights, ou
                 op0=ALU.mult,
                 op1=ALU.add,
             )
-        m2iv = const.tile([P, D], F32, name="m2iv")
+        m2iv = const.tile([P, CHANNELS], F32, name="m2iv")
         nc.gpsimd.tensor_tensor(out=m2iv[:], in0=mu[:], in1=miv32[:], op=ALU.mult)
 
         wts = {}
@@ -113,22 +114,23 @@ def tile_gmmoutlierdetector_t_kernel(tc, feats, means, log_vars, log_weights, ou
                     nc.tensor.transpose(wT[:, g, t, :], wb[:, o, g, t, :], ident_bf[:])
             wts[o] = wT
         cst_ps = ps_u.tile([P, 2, P], F32, tag="u", name="cst_ps")
-        nblk = D // P
-        for i in range(nblk):
-            nc.tensor.matmul(
-                out=cst_ps[:, 0, :], lhsT=center[:], rhs=lv[:, i * P : (i + 1) * P],
-                start=(i == 0), stop=(i == nblk - 1),
-            )
-        for i in range(nblk):
-            nc.tensor.matmul(
-                out=cst_ps[:, 1, :], lhsT=ident_f[:], rhs=m2iv[:, i * P : (i + 1) * P],
-                start=(i == 0), stop=(i == nblk - 1),
-            )
+        nblk = CHANNELS // P
+        for half, lhsT, rhs in ((0, center, lv), (1, ident_f, m2iv)):
+            for i in range(nblk):
+                nc.tensor.matmul(
+                    out=cst_ps[:, half, :],
+                    lhsT=lhsT[:],
+                    rhs=rhs[:, i * P : (i + 1) * P],
+                    start=(i == 0),
+                    stop=(i == nblk - 1),
+                )
         wg = const.tile([P, 2 * G, P, PACK], BF16, name="wg", align_bytes=64)
         wc = const.tile([P, 2 * G * P], U32, name="wc", align_bytes=64)
         ws = const.tile([P, 2 * G * P], U8, name="ws", align_bytes=64)
-        psum3 = const.tile([P, 1], F32, name="psum3")
+        csum = const.tile([P, 1], F32, name="csum")
         ybias = const.tile([P, 1], F32, name="ybias")
+        tops = const.tile([P, P], F32, name="tops")
+        tots = const.tile([P, P], F32, name="tots")
         res = const.tile([P, P], F32, name="res")
 
         def weights_out_of_psum():
@@ -141,9 +143,9 @@ def tile_gmmoutlierdetector_t_kernel(tc, feats, means, log_vars, log_weights, ou
             nc.vector.quantize_mx(
                 out=wc[:].bitcast(FP8X4), scales=ws[:], in_=wg[:].rearrange("p a c t -> p (a c t)")
             )
-            nc.vector.tensor_reduce(out=psum3[:], in_=cst_ps[:], axis=AX.XY, op=ALU.add)
+            nc.vector.tensor_reduce(out=csum[:], in_=cst_ps[:], axis=AX.XY, op=ALU.add)
             nc.vector.scalar_tensor_tensor(
-                out=ybias[:], in0=psum3[:], scalar=0.5, in1=lw[:], op0=ALU.mult, op1=ALU.subtract
+                out=ybias[:], in0=csum[:], scalar=0.5, in1=lw[:], op0=ALU.mult, op1=ALU.subtract
             )
 
         def regroup(j):
@@ -154,23 +156,19 @@ def tile_gmmoutlierdetector_t_kernel(tc, feats, means, log_vars, log_weights, ou
                 )
             st["xg", j] = xg
 
-        def v_share(j):
-            return V_SHARE_LAST if j == NGRP - 1 else V_SHARE
-
         def square_scalar(j):
             x2 = work.tile([P, G, NG, PACK], BF16, tag="x2", name="x2", align_bytes=64)
             for g in range(G):
-                n = NG - v_share(j) if g == G - 1 else NG
-                if n > 0:
-                    nc.scalar.activation(
-                        out=x2[:, g, :n, :].rearrange("p (c i) t -> p c t i", i=4),
-                        in_=raw_view(j, g)[:, : n // 4],
-                        func=ACT.Square,
-                    )
+                n = NG - V_SHARE if g == G - 1 else NG
+                nc.scalar.activation(
+                    out=x2[:, g, :n, :].rearrange("p (c i) t -> p c t i", i=4),
+                    in_=raw_view(j, g)[:, : n // 4],
+                    func=ACT.Square,
+                )
             st["x2", j] = x2
 
         def square_vector(j):
-            lo = NG - v_share(j)
+            lo = NG - V_SHARE
             xv = st["xg", j][:, G - 1, lo:, :].rearrange("p n t -> p (n t)")
             nc.vector.tensor_tensor(
                 out=st["x2", j][:, G - 1, lo:, :].rearrange("p n t -> p (n t)"),
@@ -214,11 +212,10 @@ def tile_gmmoutlierdetector_t_kernel(tc, feats, means, log_vars, log_weights, ou
             st["y", j] = y
 
         def turn(j):
+            order = ident_f if j in V_SUMS else perm
             yT = ps_t.tile([P, NT, P], F32, tag="yT", name="yT")
             for i in range(NT):
-                nc.tensor.transpose(
-                    yT[:, i, :], st["y", j][:, i * P : (i + 1) * P], ident_f[:] if j in V_SUMS else perm[:]
-                )
+                nc.tensor.transpose(yT[:, i, :], st["y", j][:, i * P : (i + 1) * P], order[:])
             st["yT", j] = yT
 
         def smallest(j):
@@ -262,7 +259,7 @@ def tile_gmmoutlierdetector_t_kernel(tc, feats, means, log_vars, log_weights, ou
 
         def pair_back(q):
             sT_sb = work.tile([P, P], F32, tag="sT_sb", name="sT_sb")
-            nc.vector.tensor_copy(out=sT_sb[:], in_=st["sT", q][:])
+            nc.scalar.copy(out=sT_sb[:], in_=st["sT", q][:])
             t_lo = q * PAIR * NT
             if t_lo % TB == 0:
                 st["s", t_lo // TB] = ps_s.tile([P, TB, NCLS], F32, tag="s", name="s_ps")
@@ -283,19 +280,17 @@ def tile_gmmoutlierdetector_t_kernel(tc, feats, means, log_vars, log_weights, ou
             )
             return gs
 
-        def finish(sv, t_lo, t_hi):
-            n = t_hi - t_lo
-            top = work.tile([P, TB], F32, tag="top", name="top")
-            nc.vector.tensor_reduce(out=top[:, :n], in_=sv, axis=AX.X, op=ALU.max)
-            tot = work.tile([P, TB], F32, tag="tot", name="tot")
-            nc.vector.tensor_reduce(out=tot[:, :n], in_=sv, axis=AX.X, op=ALU.add)
+        def over_classes(sv, t_lo, t_hi):
+            nc.vector.tensor_reduce(out=tops[:, t_lo:t_hi], in_=sv, axis=AX.X, op=ALU.max)
+            nc.vector.tensor_reduce(out=tots[:, t_lo:t_hi], in_=sv, axis=AX.X, op=ALU.add)
+
+        def scores(t_lo, t_hi):
             rec = work.tile([P, TB], F32, tag="rec", name="rec")
-            nc.vector.reciprocal(out=rec[:, :n], in_=tot[:, :n])
+            nc.vector.reciprocal(out=rec[:], in_=tots[:, t_lo:t_hi])
             share = work.tile([P, TB], F32, tag="share", name="share")
-            nc.vector.tensor_tensor(out=share[:, :n], in0=top[:, :n], in1=rec[:, :n], op=ALU.mult)
+            nc.vector.tensor_tensor(out=share[:], in0=tops[:, t_lo:t_hi], in1=rec[:], op=ALU.mult)
             nc.vector.tensor_scalar(
-                out=res[:, t_lo:t_hi], in0=share[:, :n], scalar1=-1.0, scalar2=1.0,
-                op0=ALU.mult, op1=ALU.add,
+                out=res[:, t_lo:t_hi], in0=share[:], scalar1=-1.0, scalar2=1.0, op0=ALU.mult, op1=ALU.add
             )
 
         n_pairs = min(V_SUMS) // PAIR
@@ -307,8 +302,8 @@ def tile_gmmoutlierdetector_t_kernel(tc, feats, means, log_vars, log_weights, ou
             if j < NGRP:
                 regroup(j)
                 square_scalar(j)
-                if j % UG == UG - 1 and j // UG + AHEAD < NUNIT:
-                    load(j // UG + AHEAD)
+                if j % UG == UG - 1 and j // UG + RESIDENT < IMAGES:
+                    load(j // UG + RESIDENT)
             if j == 1:
                 weights_out_of_psum()
             if 0 <= j - 1 < NGRP:
@@ -326,11 +321,15 @@ def tile_gmmoutlierdetector_t_kernel(tc, feats, means, log_vars, log_weights, ou
                 quantise(j, "xg")
             if 0 <= j - 3 < NGRP:
                 smallest(j - 3)
+            held = [r for r in due if r[1] == P - TB and j < NGRP]
             for t_lo, t_hi in due:
-                finish(st["s", t_lo // TB][:, : t_hi - t_lo, :], t_lo, t_hi)
-            due = []
+                if (t_lo, t_hi) not in held:
+                    over_classes(st["s", t_lo // TB][:, : t_hi - t_lo, :], t_lo, t_hi)
+                    if t_hi % TB == 0:
+                        scores(t_lo, t_hi)
+            due = held
             for i in late:
-                finish(vector_sums(i)[:], i * NT, (i + 1) * NT)
+                over_classes(vector_sums(i)[:], i * NT, (i + 1) * NT)
             late = []
             if 0 <= j - 2 < NGRP:
                 leave_psum(j - 2)
@@ -348,6 +347,7 @@ def tile_gmmoutlierdetector_t_kernel(tc, feats, means, log_vars, log_weights, ou
                 elif (j - 3) % PAIR == PAIR - 1:
                     pair_sums((j - 3) // PAIR)
                     summed.append((j - 3) // PAIR)
+        scores(P - TB, P)
 
         resT = ps_t.tile([P, P], F32, tag="yT", name="resT")
         nc.tensor.transpose(resT[:], res[:], ident_f[:])

@@ -160,11 +160,18 @@ def tile_gmmoutlierdetector_t_kernel(tc, feats, means, log_vars, log_weights, ou
             x2 = work.tile([P, G, NG, PACK], BF16, tag="x2", name="x2", align_bytes=64)
             for g in range(G):
                 n = NG - V_SHARE if g == G - 1 else NG
-                nc.scalar.activation(
-                    out=x2[:, g, :n, :].rearrange("p (c i) t -> p c t i", i=4),
-                    in_=raw_view(j, g)[:, : n // 4],
-                    func=ACT.Square,
-                )
+                if j in (0, NGRP - 1):
+                    nc.scalar.activation(
+                        out=x2[:, g, :n, :].rearrange("p (c i) t -> p c t i", i=4),
+                        in_=raw_view(j, g)[:, : n // 4],
+                        func=ACT.Square,
+                    )
+                else:
+                    nc.scalar.activation(
+                        out=x2[:, g, :n, :].rearrange("p n t -> p (n t)"),
+                        in_=st["xg", j][:, g, :n, :].rearrange("p n t -> p (n t)"),
+                        func=ACT.Square,
+                    )
             st["x2", j] = x2
 
         def square_vector(j):

@@ -27,6 +27,7 @@ NCMP = 8
 PAIR = 2
 TB = 32
 RESIDENT = 2
+HEAD_CUTS = (0, NG, 2 * NG, PIXELS)
 V_SHARE = 64
 V_SUMS = (NGRP - 2, NGRP - 1)
 
@@ -37,6 +38,7 @@ def tile_gmmoutlierdetector_t_kernel(tc, feats, means, log_vars, log_weights, ou
     nc = tc.nc
     with ExitStack() as ctx:
         const = ctx.enter_context(tc.tile_pool(name="const", bufs=1))
+        head = ctx.enter_context(tc.tile_pool(name="head", bufs=1))
         rawp = ctx.enter_context(tc.tile_pool(name="rawp", bufs=RESIDENT))
         work = ctx.enter_context(tc.tile_pool(name="work", bufs=3))
         ps_acc = ctx.enter_context(tc.psum_pool(name="ps_acc", bufs=2))
@@ -49,28 +51,31 @@ def tile_gmmoutlierdetector_t_kernel(tc, feats, means, log_vars, log_weights, ou
         st = {}
 
         def load(u):
-            raw = rawp.tile([P, G, PACK, PIXELS], BF16, tag="raw", name="raw")
             if u == 0:
-                cuts = (0, NG, 2 * NG, PIXELS)
-                for lo, hi in zip(cuts[:-1], cuts[1:]):
+                st["raw", u] = []
+                for lo, hi in zip(HEAD_CUTS[:-1], HEAD_CUTS[1:]):
+                    piece = head.tile([P, G, PACK, hi - lo], BF16, name="piece%d" % lo)
                     for g in range(G):
                         for t in range(PACK):
-                            nc.sync.dma_start(out=raw[:, g, t, lo:hi], in_=fv[u, g, :, t, lo:hi])
+                            nc.sync.dma_start(out=piece[:, g, t, :], in_=fv[u, g, :, t, lo:hi])
+                    st["raw", u].append((lo, hi, piece))
             else:
+                raw = rawp.tile([P, G, PACK, PIXELS], BF16, tag="raw", name="raw")
                 for g in range(G):
                     nc.sync.dma_start(out=raw[:, g], in_=fv[u, g])
-            st["raw", u] = raw
+                st["raw", u] = [(0, PIXELS, raw)]
 
         def raw_view(j, g):
             n0 = (j % UG) * NG
-            return st["raw", j // UG][:, g, :, n0 : n0 + NG].rearrange("p t (c i) -> p c t i", i=4)
+            lo, piece = [(lo, piece) for lo, hi, piece in st["raw", j // UG] if lo <= n0 < hi][0]
+            return piece[:, g, :, n0 - lo : n0 - lo + NG].rearrange("p t (c i) -> p c t i", i=4)
 
         lv = const.tile([P, CHANNELS], BF16, name="lv")
         mu = const.tile([P, CHANNELS], BF16, name="mu")
         lw = const.tile([P, 1], BF16, name="lw")
         nc.scalar.dma_start(out=lv[:], in_=log_vars.rearrange("k m d -> (k m) d"))
         nc.scalar.dma_start(out=mu[:], in_=means.rearrange("k m d -> (k m) d"))
-        for u in range(RESIDENT):
+        for u in range(1 + RESIDENT):
             load(u)
 
         ident_bf = const.tile([P, P], BF16, name="ident_bf")
@@ -87,43 +92,30 @@ def tile_gmmoutlierdetector_t_kernel(tc, feats, means, log_vars, log_weights, ou
             in_=ident_f[:].rearrange("p (k m) -> p m k", m=NCMP),
         )
 
-        iv32 = const.tile([P, CHANNELS], F32, name="iv32")
-        nc.scalar.activation(out=iv32[:], in_=lv[:], func=ACT.Exp, scale=-1.0)
-        with nc.allow_non_contiguous_dma(reason="128 log weights, one to a partition"):
-            nc.scalar.dma_start(out=lw[:], in_=log_weights.rearrange("k (m o) -> (k m) o", o=1))
-        miv32 = const.tile([P, CHANNELS], F32, name="miv32")
-        nc.gpsimd.tensor_tensor(out=miv32[:], in0=mu[:], in1=iv32[:], op=ALU.mult)
-        wb = const.tile([P, 2, G, PACK, P], BF16, name="wb")
-        for o, src, factor in ((1, miv32, -2.0), (0, iv32, 1.0)):
-            nc.gpsimd.tensor_scalar(
-                out=wb[:, o],
-                in0=src[:].rearrange("c (g p t) -> c g t p", g=G, p=P, t=PACK),
-                scalar1=factor,
-                scalar2=0.0,
-                op0=ALU.mult,
-                op1=ALU.add,
-            )
-        m2iv = const.tile([P, CHANNELS], F32, name="m2iv")
-        nc.gpsimd.tensor_tensor(out=m2iv[:], in0=mu[:], in1=miv32[:], op=ALU.mult)
+        ones = const.tile([P, 1], F32, name="ones")
+        nc.vector.memset(ones[:], 1.0)
 
-        wts = {}
-        for o in (1, 0):
-            wT = ps_t.tile([P, G, PACK, P], BF16, tag="yT", name="wT")
+        turned = {}
+        for what, table in (("lv", lv), ("mu", mu)):
+            tableT = ps_t.tile([P, G, PACK, P], BF16, tag="yT", name="tableT")
+            rows = table[:].rearrange("c (g p t) -> c g t p", g=G, p=P, t=PACK)
             for g in range(G):
                 for t in range(PACK):
-                    nc.tensor.transpose(wT[:, g, t, :], wb[:, o, g, t, :], ident_bf[:])
-            wts[o] = wT
+                    nc.tensor.transpose(tableT[:, g, t, :], rows[:, g, t, :], ident_bf[:])
+            turned[what] = tableT
         cst_ps = ps_u.tile([P, 2, P], F32, tag="u", name="cst_ps")
         nblk = CHANNELS // P
-        for half, lhsT, rhs in ((0, center, lv), (1, ident_f, m2iv)):
-            for i in range(nblk):
-                nc.tensor.matmul(
-                    out=cst_ps[:, half, :],
-                    lhsT=lhsT[:],
-                    rhs=rhs[:, i * P : (i + 1) * P],
-                    start=(i == 0),
-                    stop=(i == nblk - 1),
-                )
+        for i in range(nblk):
+            nc.tensor.matmul(
+                out=cst_ps[:, 0, :],
+                lhsT=center[:],
+                rhs=lv[:, i * P : (i + 1) * P],
+                start=(i == 0),
+                stop=(i == nblk - 1),
+            )
+        ivT = const.tile([P, G, PACK, P], F32, name="ivT")
+        mivT = const.tile([P, G, PACK, P], F32, name="mivT")
+        m2T = const.tile([P, G, PACK, P], F32, name="m2T")
         wg = const.tile([P, 2 * G, P, PACK], BF16, name="wg", align_bytes=64)
         wc = const.tile([P, 2 * G * P], U32, name="wc", align_bytes=64)
         ws = const.tile([P, 2 * G * P], U8, name="ws", align_bytes=64)
@@ -133,17 +125,42 @@ def tile_gmmoutlierdetector_t_kernel(tc, feats, means, log_vars, log_weights, ou
         tots = const.tile([P, P], F32, name="tots")
         res = const.tile([P, P], F32, name="res")
 
-        def weights_out_of_psum():
-            for o in (1, 0):
-                nc.scalar.copy(
-                    out=wg[:, o * G : (o + 1) * G], in_=wts[o][:].rearrange("p g t c -> p g c t")
+        def weights_scalar():
+            nc.scalar.activation(out=ivT[:], in_=turned["lv"][:], func=ACT.Exp, scale=-1.0)
+            nc.scalar.activation(
+                out=wg[:, 0:G], in_=turned["lv"][:].rearrange("p g t c -> p g c t"), func=ACT.Exp, scale=-1.0
+            )
+            with nc.allow_non_contiguous_dma(reason="128 log weights, one to a partition"):
+                nc.scalar.dma_start(out=lw[:], in_=log_weights.rearrange("k (m o) -> (k m) o", o=1))
+
+        def weights_vector():
+            nc.vector.tensor_tensor(out=mivT[:], in0=turned["mu"][:], in1=ivT[:], op=ALU.mult)
+            nc.vector.tensor_scalar(
+                out=wg[:, G : 2 * G],
+                in0=mivT[:].rearrange("p g t c -> p g c t"),
+                scalar1=-2.0,
+                scalar2=None,
+                op0=ALU.mult,
+            )
+            nc.vector.tensor_tensor(out=m2T[:], in0=turned["mu"][:], in1=mivT[:], op=ALU.mult)
+            for i in range(nblk):
+                nc.tensor.matmul(
+                    out=cst_ps[:, 1, 0:1],
+                    lhsT=m2T[:, i // PACK, i % PACK, :],
+                    rhs=ones[:],
+                    start=(i == 0),
+                    stop=(i == nblk - 1),
                 )
 
         def weights_quantise():
             nc.vector.quantize_mx(
                 out=wc[:].bitcast(FP8X4), scales=ws[:], in_=wg[:].rearrange("p a c t -> p (a c t)")
             )
-            nc.vector.tensor_reduce(out=csum[:], in_=cst_ps[:], axis=AX.XY, op=ALU.add)
+
+        def constants():
+            nc.vector.tensor_reduce(
+                out=csum[:], in_=cst_ps[:].rearrange("p a c -> p (a c)")[:, : P + 1], axis=AX.X, op=ALU.add
+            )
             nc.vector.scalar_tensor_tensor(
                 out=ybias[:], in0=csum[:], scalar=0.5, in1=lw[:], op0=ALU.mult, op1=ALU.subtract
             )
@@ -309,18 +326,21 @@ def tile_gmmoutlierdetector_t_kernel(tc, feats, means, log_vars, log_weights, ou
             if j < NGRP:
                 regroup(j)
                 square_scalar(j)
-                if j % UG == UG - 1 and j // UG + RESIDENT < IMAGES:
+                if j % UG == UG - 1 and 1 <= j // UG < IMAGES - RESIDENT:
                     load(j // UG + RESIDENT)
-            if j == 1:
-                weights_out_of_psum()
+            if j == 0:
+                weights_scalar()
             if 0 <= j - 1 < NGRP:
                 quantise(j - 1, "x2")
                 waiting.append(j - 1)
+            if j == 1:
+                weights_vector()
+                weights_quantise()
             if j < NGRP:
                 square_vector(j)
             if j == 2:
-                weights_quantise()
-            if j >= 2:
+                constants()
+            if j >= 1:
                 for i in waiting:
                     products(i)
                 waiting = []

@@ -25,11 +25,12 @@ NGRP = IMAGES * UG
 NCLS = 16
 NCMP = 8
 PAIR = 2
-TB = 32
+TB = 24
 RESIDENT = 2
 HEAD_CUTS = (0, NG, 2 * NG, PIXELS)
-V_SHARE = 64
+G_SHARE = 48
 V_SUMS = (NGRP - 2, NGRP - 1)
+assert (min(V_SUMS) * NT) % TB == 0
 
 FLOPS = 2 * 2 * (IMAGES * PIXELS) * CHANNELS * P
 
@@ -92,6 +93,10 @@ def tile_gmmoutlierdetector_t_kernel(tc, feats, means, log_vars, log_weights, ou
             in_=ident_f[:].rearrange("p (k m) -> p m k", m=NCMP),
         )
 
+        tile_of = const.tile([P, PAIR * NT], F32, name="tile_of")
+        nc.vector.tensor_reduce(
+            out=tile_of[:], in_=ident_f[:].rearrange("p (i k) -> p i k", k=NCLS), axis=AX.X, op=ALU.add
+        )
         ones = const.tile([P, 1], F32, name="ones")
         nc.vector.memset(ones[:], 1.0)
 
@@ -176,7 +181,7 @@ def tile_gmmoutlierdetector_t_kernel(tc, feats, means, log_vars, log_weights, ou
         def square_scalar(j):
             x2 = work.tile([P, G, NG, PACK], BF16, tag="x2", name="x2", align_bytes=64)
             for g in range(G):
-                n = NG - V_SHARE if g == G - 1 else NG
+                n = NG - G_SHARE if g == 0 else NG
                 if j in (0, NGRP - 1):
                     nc.scalar.activation(
                         out=x2[:, g, :n, :].rearrange("p (c i) t -> p c t i", i=4),
@@ -191,14 +196,11 @@ def tile_gmmoutlierdetector_t_kernel(tc, feats, means, log_vars, log_weights, ou
                     )
             st["x2", j] = x2
 
-        def square_vector(j):
-            lo = NG - V_SHARE
-            xv = st["xg", j][:, G - 1, lo:, :].rearrange("p n t -> p (n t)")
-            nc.vector.tensor_tensor(
-                out=st["x2", j][:, G - 1, lo:, :].rearrange("p n t -> p (n t)"),
-                in0=xv,
-                in1=xv,
-                op=ALU.mult,
+        def square_gpsimd(j):
+            lo = NG - G_SHARE
+            xv = st["xg", j][:, 0, lo:, :].rearrange("p n t -> p (n t)")
+            nc.gpsimd.tensor_tensor(
+                out=st["x2", j][:, 0, lo:, :].rearrange("p n t -> p (n t)"), in0=xv, in1=xv, op=ALU.mult
             )
 
         def quantise(j, what):
@@ -286,12 +288,17 @@ def tile_gmmoutlierdetector_t_kernel(tc, feats, means, log_vars, log_weights, ou
             nc.scalar.copy(out=sT_sb[:], in_=st["sT", q][:])
             t_lo = q * PAIR * NT
             if t_lo % TB == 0:
-                st["s", t_lo // TB] = ps_s.tile([P, TB, NCLS], F32, tag="s", name="s_ps")
+                st["s", t_lo // TB] = ps_s.tile([P, NG], F32, tag="s", name="s_ps")
             slot = t_lo % TB
             nc.tensor.transpose(
-                st["s", t_lo // TB][:, slot : slot + PAIR * NT, :].rearrange("p i k -> p (i k)"),
-                sT_sb[:],
-                ident_f[:],
+                st["s", t_lo // TB][:, slot * NCLS : (slot + PAIR * NT) * NCLS], sT_sb[:], ident_f[:]
+            )
+            nc.tensor.matmul(
+                out=st["s", t_lo // TB][:, TB * NCLS + slot : TB * NCLS + slot + PAIR * NT],
+                lhsT=sT_sb[:],
+                rhs=tile_of[:],
+                start=True,
+                stop=True,
             )
 
         def vector_sums(j):
@@ -304,30 +311,48 @@ def tile_gmmoutlierdetector_t_kernel(tc, feats, means, log_vars, log_weights, ou
             )
             return gs
 
-        def over_classes(sv, t_lo, t_hi):
+        def shares(sv, totals, t_lo, t_hi):
             nc.vector.tensor_reduce(out=tops[:, t_lo:t_hi], in_=sv, axis=AX.X, op=ALU.max)
-            nc.vector.tensor_reduce(out=tots[:, t_lo:t_hi], in_=sv, axis=AX.X, op=ALU.add)
-
-        def scores(t_lo, t_hi):
             rec = work.tile([P, TB], F32, tag="rec", name="rec")
-            nc.vector.reciprocal(out=rec[:], in_=tots[:, t_lo:t_hi])
-            share = work.tile([P, TB], F32, tag="share", name="share")
-            nc.vector.tensor_tensor(out=share[:], in0=tops[:, t_lo:t_hi], in1=rec[:], op=ALU.mult)
-            nc.vector.tensor_scalar(
-                out=res[:, t_lo:t_hi], in0=share[:], scalar1=-1.0, scalar2=1.0, op0=ALU.mult, op1=ALU.add
+            nc.vector.reciprocal(out=rec[:, : t_hi - t_lo], in_=totals)
+            nc.vector.tensor_tensor(
+                out=res[:, t_lo:t_hi], in0=tops[:, t_lo:t_hi], in1=rec[:, : t_hi - t_lo], op=ALU.mult
             )
 
-        n_pairs = min(V_SUMS) // PAIR
         waiting = []
         summed = []
         due = []
         late = []
+
+        def reductions(j):
+            if 0 <= j - 3 < NGRP:
+                smallest(j - 3)
+            held = [r for r in due if r[1] == min(V_SUMS) * NT - TB and j < NGRP]
+            for t_lo, t_hi in due:
+                if (t_lo, t_hi) not in held:
+                    bank = st["s", t_lo // TB]
+                    shares(
+                        bank[:, : TB * NCLS].rearrange("p (i k) -> p i k", k=NCLS),
+                        bank[:, TB * NCLS : TB * (NCLS + 1)],
+                        t_lo,
+                        t_hi,
+                    )
+            due.clear()
+            due.extend(held)
+            for i in late:
+                gs = vector_sums(i)
+                nc.vector.tensor_reduce(out=tots[:, i * NT : (i + 1) * NT], in_=gs[:], axis=AX.X, op=ALU.add)
+                shares(gs[:], tots[:, i * NT : (i + 1) * NT], i * NT, (i + 1) * NT)
+            late.clear()
+
         for j in range(NGRP + 4):
             if j < NGRP:
                 regroup(j)
                 square_scalar(j)
+                square_gpsimd(j)
                 if j % UG == UG - 1 and 1 <= j // UG < IMAGES - RESIDENT:
                     load(j // UG + RESIDENT)
+                reductions(j)
             if j == 0:
                 weights_scalar()
             if 0 <= j - 1 < NGRP:
@@ -336,8 +361,6 @@ def tile_gmmoutlierdetector_t_kernel(tc, feats, means, log_vars, log_weights, ou
             if j == 1:
                 weights_vector()
                 weights_quantise()
-            if j < NGRP:
-                square_vector(j)
             if j == 2:
                 constants()
             if j >= 1:
@@ -346,26 +369,16 @@ def tile_gmmoutlierdetector_t_kernel(tc, feats, means, log_vars, log_weights, ou
                 waiting = []
             if j < NGRP:
                 quantise(j, "xg")
-            if 0 <= j - 3 < NGRP:
-                smallest(j - 3)
-            held = [r for r in due if r[1] == P - TB and j < NGRP]
-            for t_lo, t_hi in due:
-                if (t_lo, t_hi) not in held:
-                    over_classes(st["s", t_lo // TB][:, : t_hi - t_lo, :], t_lo, t_hi)
-                    if t_hi % TB == 0:
-                        scores(t_lo, t_hi)
-            due = held
-            for i in late:
-                over_classes(vector_sums(i)[:], i * NT, (i + 1) * NT)
-            late = []
+            else:
+                reductions(j)
             if 0 <= j - 2 < NGRP:
                 leave_psum(j - 2)
                 turn(j - 2)
             for q in summed:
                 pair_back(q)
                 t_hi = (q + 1) * PAIR * NT
-                if t_hi % TB == 0 or q == n_pairs - 1:
-                    due.append((t_hi - 1 - (t_hi - 1) % TB, t_hi))
+                if t_hi % TB == 0:
+                    due.append((t_hi - TB, t_hi))
             summed = []
             if 0 <= j - 3 < NGRP:
                 exponent(j - 3)
@@ -374,10 +387,10 @@ def tile_gmmoutlierdetector_t_kernel(tc, feats, means, log_vars, log_weights, ou
                 elif (j - 3) % PAIR == PAIR - 1:
                     pair_sums((j - 3) // PAIR)
                     summed.append((j - 3) // PAIR)
-        scores(P - TB, P)
-
         resT = ps_t.tile([P, P], F32, tag="yT", name="resT")
         nc.tensor.transpose(resT[:], res[:], ident_f[:])
         res_sb = const.tile([P, P], F32, name="res_sb")
-        nc.vector.tensor_copy(out=res_sb[:], in_=resT[:])
+        nc.vector.tensor_scalar(
+            out=res_sb[:], in0=resT[:], scalar1=-1.0, scalar2=1.0, op0=ALU.mult, op1=ALU.add
+        )
         nc.sync.dma_start(out=out.rearrange("b (x y) w -> (b x) (y w)", y=2), in_=res_sb[:])

@@ -29,6 +29,7 @@ TB = 24
 RESIDENT = 2
 HEAD_CUTS = (0, NG, 2 * NG, PIXELS)
 G_SHARE = 48
+V_SHARE = 32
 V_SUMS = (NGRP - 2, NGRP - 1)
 assert (min(V_SUMS) * NT) % TB == 0
 
@@ -181,7 +182,7 @@ def tile_gmmoutlierdetector_t_kernel(tc, feats, means, log_vars, log_weights, ou
         def square_scalar(j):
             x2 = work.tile([P, G, NG, PACK], BF16, tag="x2", name="x2", align_bytes=64)
             for g in range(G):
-                n = NG - G_SHARE if g == 0 else NG
+                n = NG - G_SHARE if g == 0 else NG - V_SHARE
                 if j in (0, NGRP - 1):
                     nc.scalar.activation(
                         out=x2[:, g, :n, :].rearrange("p (c i) t -> p c t i", i=4),
@@ -201,6 +202,13 @@ def tile_gmmoutlierdetector_t_kernel(tc, feats, means, log_vars, log_weights, ou
             xv = st["xg", j][:, 0, lo:, :].rearrange("p n t -> p (n t)")
             nc.gpsimd.tensor_tensor(
                 out=st["x2", j][:, 0, lo:, :].rearrange("p n t -> p (n t)"), in0=xv, in1=xv, op=ALU.mult
+            )
+
+        def square_vector(j):
+            lo = NG - V_SHARE
+            xv = st["xg", j][:, G - 1, lo:, :].rearrange("p n t -> p (n t)")
+            nc.vector.tensor_tensor(
+                out=st["x2", j][:, G - 1, lo:, :].rearrange("p n t -> p (n t)"), in0=xv, in1=xv, op=ALU.mult
             )
 
         def quantise(j, what):
@@ -361,6 +369,8 @@ def tile_gmmoutlierdetector_t_kernel(tc, feats, means, log_vars, log_weights, ou
             if j == 1:
                 weights_vector()
                 weights_quantise()
+            if j < NGRP:
+                square_vector(j)
             if j == 2:
                 constants()
             if j >= 1:

@@ -28,8 +28,9 @@ PAIR = 2
 TB = 24
 RESIDENT = 2
 HEAD_CUTS = (0, NG, 2 * NG, PIXELS)
-G_SHARE = 48
-V_SHARE = 32
+T_SHARE = 192
+G_SHARE = 160
+V_SHARE = 112
 V_SUMS = (NGRP - 2, NGRP - 1)
 assert (min(V_SUMS) * NT) % TB == 0
 
@@ -43,9 +44,11 @@ def tile_gmmoutlierdetector_t_kernel(tc, feats, means, log_vars, log_weights, ou
         head = ctx.enter_context(tc.tile_pool(name="head", bufs=1))
         rawp = ctx.enter_context(tc.tile_pool(name="rawp", bufs=RESIDENT))
         work = ctx.enter_context(tc.tile_pool(name="work", bufs=3))
+        xgp = ctx.enter_context(tc.tile_pool(name="xgp", bufs=2))
         ps_acc = ctx.enter_context(tc.psum_pool(name="ps_acc", bufs=2))
         ps_t = ctx.enter_context(tc.psum_pool(name="ps_t", bufs=3))
-        ps_s = ctx.enter_context(tc.psum_pool(name="ps_s", bufs=2))
+        ps_s = ctx.enter_context(tc.psum_pool(name="ps_s", bufs=1))
+        ps_x = ctx.enter_context(tc.psum_pool(name="ps_x", bufs=1))
         ps_u = ctx.enter_context(tc.psum_pool(name="ps_u", bufs=1))
         ctx.enter_context(tc.manual_schedule())
 
@@ -171,18 +174,58 @@ def tile_gmmoutlierdetector_t_kernel(tc, feats, means, log_vars, log_weights, ou
                 out=ybias[:], in0=csum[:], scalar=0.5, in1=lw[:], op0=ALU.mult, op1=ALU.subtract
             )
 
-        def regroup(j):
-            xg = work.tile([P, G, NG, PACK], BF16, tag="xg", name="xg", align_bytes=64)
-            for g in range(G):
-                nc.vector.tensor_copy(
-                    out=xg[:, g].rearrange("p (c i) t -> p c t i", i=4), in_=raw_view(j, g)
-                )
+        def rows(j):
+            n0 = (j % UG) * NG
+            lo, piece = [(lo, piece) for lo, hi, piece in st["raw", j // UG] if lo <= n0 < hi][0]
+            return piece, n0 - lo
+
+        V_END = NG - T_SHARE - G_SHARE
+        G_END = NG - T_SHARE
+
+        def regroup_gpsimd(j):
+            xg = xgp.tile([P, G, NG, PACK], BF16, tag="xg", name="xg", align_bytes=64)
+            piece, a = rows(j)
+            nc.gpsimd.tensor_scalar(
+                out=xg[:, G - 1, V_END:G_END, :],
+                in0=piece[:, G - 1, :, a + V_END : a + G_END].rearrange("p t n -> p n t"),
+                scalar1=1.0,
+                scalar2=0.0,
+                op0=ALU.mult,
+                op1=ALU.add,
+            )
             st["xg", j] = xg
+
+        def regroup(j, g):
+            n = V_END if g == G - 1 else NG
+            nc.vector.tensor_copy(
+                out=st["xg", j][:, g, :n, :].rearrange("p (c i) t -> p c t i", i=4), in_=raw_view(j, g)[:, : n // 4]
+            )
+
+        def regroup_tensor(j):
+            piece, a = rows(j)
+            xp = ps_x.tile([P, T_SHARE, PACK], BF16, tag="xp", name="xp")
+            for lo in range(0, T_SHARE, P):
+                hi = min(lo + P, T_SHARE)
+                nc.tensor.matmul(
+                    out=xp[:, lo:hi, :].rearrange("p n t -> p (n t)"),
+                    lhsT=ident_bf[:],
+                    rhs=piece[:, G - 1, :, a + G_END + lo : a + G_END + hi].rearrange("p t n -> p n t"),
+                    start=True,
+                    stop=True,
+                )
+            st["xp", j] = xp
+
+        def regroup_out_of_psum(j):
+            nc.vector.tensor_copy(
+                out=st["xg", j][:, G - 1, G_END:, :].rearrange("p n t -> p (n t)"),
+                in_=st["xp", j][:].rearrange("p n t -> p (n t)"),
+            )
 
         def square_scalar(j):
             x2 = work.tile([P, G, NG, PACK], BF16, tag="x2", name="x2", align_bytes=64)
+            st["x2", j] = x2
             for g in range(G):
-                n = NG - G_SHARE if g == 0 else NG - V_SHARE
+                n = NG - V_SHARE if g == 0 else NG
                 if j in (0, NGRP - 1):
                     nc.scalar.activation(
                         out=x2[:, g, :n, :].rearrange("p (c i) t -> p c t i", i=4),
@@ -195,20 +238,12 @@ def tile_gmmoutlierdetector_t_kernel(tc, feats, means, log_vars, log_weights, ou
                         in_=st["xg", j][:, g, :n, :].rearrange("p n t -> p (n t)"),
                         func=ACT.Square,
                     )
-            st["x2", j] = x2
-
-        def square_gpsimd(j):
-            lo = NG - G_SHARE
-            xv = st["xg", j][:, 0, lo:, :].rearrange("p n t -> p (n t)")
-            nc.gpsimd.tensor_tensor(
-                out=st["x2", j][:, 0, lo:, :].rearrange("p n t -> p (n t)"), in0=xv, in1=xv, op=ALU.mult
-            )
 
         def square_vector(j):
             lo = NG - V_SHARE
-            xv = st["xg", j][:, G - 1, lo:, :].rearrange("p n t -> p (n t)")
+            xv = st["xg", j][:, 0, lo:, :].rearrange("p n t -> p (n t)")
             nc.vector.tensor_tensor(
-                out=st["x2", j][:, G - 1, lo:, :].rearrange("p n t -> p (n t)"), in0=xv, in1=xv, op=ALU.mult
+                out=st["x2", j][:, 0, lo:, :].rearrange("p n t -> p (n t)"), in0=xv, in1=xv, op=ALU.mult
             )
 
         def quantise(j, what):
@@ -327,45 +362,51 @@ def tile_gmmoutlierdetector_t_kernel(tc, feats, means, log_vars, log_weights, ou
                 out=res[:, t_lo:t_hi], in0=tops[:, t_lo:t_hi], in1=rec[:, : t_hi - t_lo], op=ALU.mult
             )
 
-        waiting = []
         summed = []
         due = []
         late = []
 
         def reductions(j):
+            if j < NGRP:
+                regroup_out_of_psum(j)
             if 0 <= j - 3 < NGRP:
                 smallest(j - 3)
-            held = [r for r in due if r[1] == min(V_SUMS) * NT - TB and j < NGRP]
             for t_lo, t_hi in due:
-                if (t_lo, t_hi) not in held:
-                    bank = st["s", t_lo // TB]
-                    shares(
-                        bank[:, : TB * NCLS].rearrange("p (i k) -> p i k", k=NCLS),
-                        bank[:, TB * NCLS : TB * (NCLS + 1)],
-                        t_lo,
-                        t_hi,
-                    )
+                bank = st["s", t_lo // TB]
+                shares(
+                    bank[:, : TB * NCLS].rearrange("p (i k) -> p i k", k=NCLS),
+                    bank[:, TB * NCLS : TB * (NCLS + 1)],
+                    t_lo,
+                    t_hi,
+                )
             due.clear()
-            due.extend(held)
             for i in late:
                 gs = vector_sums(i)
                 nc.vector.tensor_reduce(out=tots[:, i * NT : (i + 1) * NT], in_=gs[:], axis=AX.X, op=ALU.add)
                 shares(gs[:], tots[:, i * NT : (i + 1) * NT], i * NT, (i + 1) * NT)
             late.clear()
 
+        regroup_gpsimd(0)
+        regroup_tensor(0)
         for j in range(NGRP + 4):
             if j < NGRP:
-                regroup(j)
+                regroup(j, 0)
+            if 0 <= j - 1 < NGRP:
+                quantise(j - 1, "xg")
+            if j < NGRP:
+                if j + 1 < NGRP:
+                    regroup_gpsimd(j + 1)
+                regroup(j, 1)
+                reductions(j)
+                if j + 1 < NGRP:
+                    regroup_tensor(j + 1)
                 square_scalar(j)
-                square_gpsimd(j)
                 if j % UG == UG - 1 and 1 <= j // UG < IMAGES - RESIDENT:
                     load(j // UG + RESIDENT)
-                reductions(j)
             if j == 0:
                 weights_scalar()
             if 0 <= j - 1 < NGRP:
                 quantise(j - 1, "x2")
-                waiting.append(j - 1)
             if j == 1:
                 weights_vector()
                 weights_quantise()
@@ -373,13 +414,9 @@ def tile_gmmoutlierdetector_t_kernel(tc, feats, means, log_vars, log_weights, ou
                 square_vector(j)
             if j == 2:
                 constants()
-            if j >= 1:
-                for i in waiting:
-                    products(i)
-                waiting = []
-            if j < NGRP:
-                quantise(j, "xg")
-            else:
+            if 0 <= j - 1 < NGRP:
+                products(j - 1)
+            if j >= NGRP:
                 reductions(j)
             if 0 <= j - 2 < NGRP:
                 leave_psum(j - 2)

@@ -31,8 +31,10 @@ HEAD_CUTS = (0, NG, 2 * NG, PIXELS)
 T_SHARE = 192
 G_SHARE = 160
 V_SHARE = 112
+ALL_SCALAR = 6
 V_SUMS = (NGRP - 2, NGRP - 1)
 assert (min(V_SUMS) * NT) % TB == 0
+LAST_PARTS = 2
 
 FLOPS = 2 * 2 * (IMAGES * PIXELS) * CHANNELS * P
 
@@ -64,6 +66,9 @@ def tile_gmmoutlierdetector_t_kernel(tc, feats, means, log_vars, log_weights, ou
                         for t in range(PACK):
                             nc.sync.dma_start(out=piece[:, g, t, :], in_=fv[u, g, :, t, lo:hi])
                     st["raw", u].append((lo, hi, piece))
+                    if lo == 0:
+                        nc.sync.dma_start(out=lv[:], in_=log_vars.rearrange("k m d -> (k m) d"))
+                        nc.sync.dma_start(out=mu[:], in_=means.rearrange("k m d -> (k m) d"))
             else:
                 raw = rawp.tile([P, G, PACK, PIXELS], BF16, tag="raw", name="raw")
                 for g in range(G):
@@ -78,10 +83,13 @@ def tile_gmmoutlierdetector_t_kernel(tc, feats, means, log_vars, log_weights, ou
         lv = const.tile([P, CHANNELS], BF16, name="lv")
         mu = const.tile([P, CHANNELS], BF16, name="mu")
         lw = const.tile([P, 1], BF16, name="lw")
-        nc.scalar.dma_start(out=lv[:], in_=log_vars.rearrange("k m d -> (k m) d"))
-        nc.scalar.dma_start(out=mu[:], in_=means.rearrange("k m d -> (k m) d"))
         for u in range(1 + RESIDENT):
             load(u)
+
+        ones = const.tile([P, 1], F32, name="ones")
+        nc.vector.memset(ones[:], 1.0)
+        warm = const.tile([P, 1], F32, name="warm")
+        nc.scalar.activation(out=warm[:], in_=ones[:], func=ACT.Exp)
 
         ident_bf = const.tile([P, P], BF16, name="ident_bf")
         make_identity(nc, ident_bf[:])
@@ -101,27 +109,29 @@ def tile_gmmoutlierdetector_t_kernel(tc, feats, means, log_vars, log_weights, ou
         nc.vector.tensor_reduce(
             out=tile_of[:], in_=ident_f[:].rearrange("p (i k) -> p i k", k=NCLS), axis=AX.X, op=ALU.add
         )
-        ones = const.tile([P, 1], F32, name="ones")
-        nc.vector.memset(ones[:], 1.0)
 
         turned = {}
-        for what, table in (("lv", lv), ("mu", mu)):
-            tableT = ps_t.tile([P, G, PACK, P], BF16, tag="yT", name="tableT")
-            rows = table[:].rearrange("c (g p t) -> c g t p", g=G, p=P, t=PACK)
-            for g in range(G):
-                for t in range(PACK):
-                    nc.tensor.transpose(tableT[:, g, t, :], rows[:, g, t, :], ident_bf[:])
-            turned[what] = tableT
-        cst_ps = ps_u.tile([P, 2, P], F32, tag="u", name="cst_ps")
         nblk = CHANNELS // P
-        for i in range(nblk):
-            nc.tensor.matmul(
-                out=cst_ps[:, 0, :],
-                lhsT=center[:],
-                rhs=lv[:, i * P : (i + 1) * P],
-                start=(i == 0),
-                stop=(i == nblk - 1),
-            )
+
+        def turn_tables():
+            for what, table in (("lv", lv), ("mu", mu)):
+                tableT = ps_t.tile([P, G, PACK, P], BF16, tag="yT", name="tableT")
+                rows = table[:].rearrange("c (g p t) -> c g t p", g=G, p=P, t=PACK)
+                for g in range(G):
+                    for t in range(PACK):
+                        nc.tensor.transpose(tableT[:, g, t, :], rows[:, g, t, :], ident_bf[:])
+                turned[what] = tableT
+            cst_ps = ps_u.tile([P, 2, P], F32, tag="u", name="cst_ps")
+            turned["cst"] = cst_ps
+            for i in range(nblk):
+                nc.tensor.matmul(
+                    out=cst_ps[:, 0, :],
+                    lhsT=center[:],
+                    rhs=lv[:, i * P : (i + 1) * P],
+                    start=(i == 0),
+                    stop=(i == nblk - 1),
+                )
+
         ivT = const.tile([P, G, PACK, P], F32, name="ivT")
         mivT = const.tile([P, G, PACK, P], F32, name="mivT")
         m2T = const.tile([P, G, PACK, P], F32, name="m2T")
@@ -131,19 +141,23 @@ def tile_gmmoutlierdetector_t_kernel(tc, feats, means, log_vars, log_weights, ou
         csum = const.tile([P, 1], F32, name="csum")
         ybias = const.tile([P, 1], F32, name="ybias")
         tops = const.tile([P, P], F32, name="tops")
-        tots = const.tile([P, P], F32, name="tots")
+        gs = const.tile([P, len(V_SUMS) * NT, NCLS], F32, name="gs")
         res = const.tile([P, P], F32, name="res")
 
-        def weights_scalar():
+        def weights_exp():
             nc.scalar.activation(out=ivT[:], in_=turned["lv"][:], func=ACT.Exp, scale=-1.0)
+
+        def weights_exp_words():
             nc.scalar.activation(
                 out=wg[:, 0:G], in_=turned["lv"][:].rearrange("p g t c -> p g c t"), func=ACT.Exp, scale=-1.0
             )
             with nc.allow_non_contiguous_dma(reason="128 log weights, one to a partition"):
                 nc.scalar.dma_start(out=lw[:], in_=log_weights.rearrange("k (m o) -> (k m) o", o=1))
 
-        def weights_vector():
+        def weights_product():
             nc.vector.tensor_tensor(out=mivT[:], in0=turned["mu"][:], in1=ivT[:], op=ALU.mult)
+
+        def weights_words():
             nc.vector.tensor_scalar(
                 out=wg[:, G : 2 * G],
                 in0=mivT[:].rearrange("p g t c -> p g c t"),
@@ -151,10 +165,12 @@ def tile_gmmoutlierdetector_t_kernel(tc, feats, means, log_vars, log_weights, ou
                 scalar2=None,
                 op0=ALU.mult,
             )
+
+        def weights_constant():
             nc.vector.tensor_tensor(out=m2T[:], in0=turned["mu"][:], in1=mivT[:], op=ALU.mult)
             for i in range(nblk):
                 nc.tensor.matmul(
-                    out=cst_ps[:, 1, 0:1],
+                    out=turned["cst"][:, 1, 0:1],
                     lhsT=m2T[:, i // PACK, i % PACK, :],
                     rhs=ones[:],
                     start=(i == 0),
@@ -168,7 +184,7 @@ def tile_gmmoutlierdetector_t_kernel(tc, feats, means, log_vars, log_weights, ou
 
         def constants():
             nc.vector.tensor_reduce(
-                out=csum[:], in_=cst_ps[:].rearrange("p a c -> p (a c)")[:, : P + 1], axis=AX.X, op=ALU.add
+                out=csum[:], in_=turned["cst"][:].rearrange("p a c -> p (a c)")[:, : P + 1], axis=AX.X, op=ALU.add
             )
             nc.vector.scalar_tensor_tensor(
                 out=ybias[:], in0=csum[:], scalar=0.5, in1=lw[:], op0=ALU.mult, op1=ALU.subtract
@@ -225,13 +241,15 @@ def tile_gmmoutlierdetector_t_kernel(tc, feats, means, log_vars, log_weights, ou
             x2 = work.tile([P, G, NG, PACK], BF16, tag="x2", name="x2", align_bytes=64)
             st["x2", j] = x2
             for g in range(G):
-                n = NG - V_SHARE if g == 0 else NG
+                n = NG - V_SHARE if g == 0 and j >= ALL_SCALAR else NG
                 if j in (0, NGRP - 1):
                     nc.scalar.activation(
                         out=x2[:, g, :n, :].rearrange("p (c i) t -> p c t i", i=4),
                         in_=raw_view(j, g)[:, : n // 4],
                         func=ACT.Square,
                     )
+                    if j == g == 0:
+                        weights_exp()
                 else:
                     nc.scalar.activation(
                         out=x2[:, g, :n, :].rearrange("p n t -> p (n t)"),
@@ -256,61 +274,80 @@ def tile_gmmoutlierdetector_t_kernel(tc, feats, means, log_vars, log_weights, ou
             )
             st[what + "q", j] = (codes, scales)
 
-        def products(j):
-            acc = ps_acc.tile([P, NG], F32, tag="acc", name="acc")
+        def quantise_part(j, h, what):
+            if h == 0:
+                codes = work.tile([P, G * NG], U32, tag=what + "c", name="codes", align_bytes=64)
+                scales = work.tile([P, G * NG], U8, tag=what + "s", name="scales", align_bytes=64)
+                st[what + "q", j] = (codes, scales)
+            codes, scales = st[what + "q", j]
+            n = NG // LAST_PARTS
+            for g in range(G):
+                c = slice(g * NG + h * n, g * NG + (h + 1) * n)
+                nc.vector.quantize_mx(
+                    out=codes[:, c].bitcast(FP8X4),
+                    scales=scales[:, c],
+                    in_=st[what, j][:, g, h * n : (h + 1) * n, :].rearrange("p n t -> p (n t)"),
+                )
+
+        def products(j, h=0, parts=1):
+            n = NG // parts
+            acc = ps_acc.tile([P, n], F32, tag="acc", name="acc")
             passes = [(1, g, "xgq") for g in range(G)] + [(0, g, "x2q") for g in range(G)]
             for idx, (o, g, what) in enumerate(passes):
                 codes, scales = st[what, j]
                 a = (o * G + g) * P
+                c = slice(g * NG + h * n, g * NG + (h + 1) * n)
                 nc.tensor.matmul_mx(
                     out=acc[:],
                     lhsT=wc[:, a : a + P].bitcast(FP8X4),
                     lhsT_scale=ws[:, a : a + P],
-                    rhs=codes[:, g * NG : (g + 1) * NG].bitcast(FP8X4),
-                    rhs_scale=scales[:, g * NG : (g + 1) * NG],
+                    rhs=codes[:, c].bitcast(FP8X4),
+                    rhs_scale=scales[:, c],
                     start=(idx == 0),
                     stop=(idx == len(passes) - 1),
                 )
-            st["acc", j] = acc
+            st["acc", j, h] = acc
 
-        def leave_psum(j):
-            y = work.tile([P, NG], F32, tag="y", name="y")
+        def leave_psum(j, h=0, parts=1):
+            y = work.tile([P, NG // parts], F32, tag="y", name="y")
             nc.scalar.activation(
-                out=y[:], in_=st["acc", j][:], func=ACT.Identity, bias=ybias[:, 0:1], scale=0.5
+                out=y[:], in_=st["acc", j, h][:], func=ACT.Identity, bias=ybias[:, 0:1], scale=0.5
             )
-            st["y", j] = y
+            st["y", j, h] = y
 
-        def turn(j):
+        def turn(j, h=0, parts=1):
             order = ident_f if j in V_SUMS else perm
-            yT = ps_t.tile([P, NT, P], F32, tag="yT", name="yT")
-            for i in range(NT):
-                nc.tensor.transpose(yT[:, i, :], st["y", j][:, i * P : (i + 1) * P], order[:])
-            st["yT", j] = yT
+            nt = NT // parts
+            yT = ps_t.tile([P, nt, P], F32, tag="yT", name="yT")
+            for i in range(nt):
+                nc.tensor.transpose(yT[:, i, :], st["y", j, h][:, i * P : (i + 1) * P], order[:])
+            st["yT", j, h] = yT
 
-        def smallest(j):
-            mn = work.tile([P, NT], F32, tag="mn", name="mn")
-            nc.vector.tensor_reduce(out=mn[:], in_=st["yT", j][:], axis=AX.X, op=ALU.min)
-            st["mn", j] = mn
+        def smallest(j, h=0, parts=1):
+            mn = work.tile([P, NT // parts], F32, tag="mn", name="mn")
+            nc.vector.tensor_reduce(out=mn[:], in_=st["yT", j, h][:], axis=AX.X, op=ALU.min)
+            st["mn", j, h] = mn
 
-        def exponent(j):
+        def exponent(j, h=0, parts=1):
+            nt = NT // parts
+            yT = st["yT", j, h]
             if j in V_SUMS:
-                e = work.tile([P, NT, P], F32, tag="e", name="e")
-                outs = [e[:, i, :] for i in range(NT)]
-                ins = [st["yT", j][:, i, :] for i in range(NT)]
-                st["e", j] = e
+                e = work.tile([P, nt, P], F32, tag="e", name="e")
+                st["e", j, h] = e
+                outs = [e[:, i, :] for i in range(nt)]
+                ins = [yT[:, i, :] for i in range(nt)]
             else:
                 if j % PAIR == 0:
-                    st["eb", j // PAIR] = work.tile(
-                        [P, NCMP, PAIR * NT, NCLS], F32, tag="eb", name="eb"
-                    )
-                eb = st["eb", j // PAIR]
-                outs = [eb[:, :, (j % PAIR) * NT + i, :] for i in range(NT)]
-                ins = [
-                    st["yT", j][:, i, :].rearrange("p (m k) -> p m k", m=NCMP) for i in range(NT)
-                ]
-            for i in range(NT):
+                    st["eb", j // PAIR] = work.tile([P, NCMP, PAIR * NT, NCLS], F32, tag="eb", name="eb")
+                outs = [st["eb", j // PAIR][:, :, (j % PAIR) * NT + i, :] for i in range(nt)]
+                ins = [yT[:, i, :].rearrange("p (m k) -> p m k", m=NCMP) for i in range(nt)]
+            for i in range(nt):
                 nc.scalar.activation(
-                    out=outs[i], in_=ins[i], func=ACT.Exp, bias=st["mn", j][:, i : i + 1], scale=-1.0
+                    out=outs[i],
+                    in_=ins[i],
+                    func=ACT.Exp,
+                    bias=st["mn", j, h][:, i : i + 1],
+                    scale=-1.0,
                 )
 
         def pair_sums(q):
@@ -344,96 +381,132 @@ def tile_gmmoutlierdetector_t_kernel(tc, feats, means, log_vars, log_weights, ou
                 stop=True,
             )
 
-        def vector_sums(j):
-            gs = work.tile([P, NT, NCLS], F32, tag="gs", name="gs")
+        def vector_sums(j, h=0, parts=1):
+            t_lo = (j - V_SUMS[0]) * NT + h * NT // parts
             nc.vector.tensor_reduce(
-                out=gs[:],
-                in_=st["e", j][:].rearrange("p i (k m) -> p i k m", m=NCMP),
+                out=gs[:, t_lo : t_lo + NT // parts, :],
+                in_=st["e", j, h][:].rearrange("p i (k m) -> p i k m", m=NCMP),
                 axis=AX.X,
                 op=ALU.add,
             )
-            return gs
 
-        def shares(sv, totals, t_lo, t_hi):
-            nc.vector.tensor_reduce(out=tops[:, t_lo:t_hi], in_=sv, axis=AX.X, op=ALU.max)
-            rec = work.tile([P, TB], F32, tag="rec", name="rec")
-            nc.vector.reciprocal(out=rec[:, : t_hi - t_lo], in_=totals)
-            nc.vector.tensor_tensor(
-                out=res[:, t_lo:t_hi], in0=tops[:, t_lo:t_hi], in1=rec[:, : t_hi - t_lo], op=ALU.mult
+        def vector_shares():
+            tots = const.tile([P, len(V_SUMS) * NT], F32, name="tots")
+            nc.vector.tensor_reduce(out=tots[:], in_=gs[:], axis=AX.X, op=ALU.add)
+            shares(gs[:], tots[:], V_SUMS[0] * NT)
+
+        def bank_shares(t_hi):
+            bank = st["s", t_hi // TB - 1]
+            shares(
+                bank[:, : TB * NCLS].rearrange("p (i k) -> p i k", k=NCLS),
+                bank[:, TB * NCLS : TB * (NCLS + 1)],
+                t_hi - TB,
             )
+
+        def shares(sv, totals, t_lo):
+            n = sv.shape[1]
+            rec = work.tile([P, TB], F32, tag="rec", name="rec")
+            nc.vector.tensor_reduce(out=tops[:, t_lo : t_lo + n], in_=sv, axis=AX.X, op=ALU.max)
+            nc.vector.reciprocal(out=rec[:, :n], in_=totals)
+            shared.append((rec, t_lo, t_lo + n))
+
+        def divide():
+            for rec, t_lo, t_hi in shared:
+                nc.vector.tensor_tensor(
+                    out=res[:, t_lo:t_hi], in0=tops[:, t_lo:t_hi], in1=rec[:, : t_hi - t_lo], op=ALU.mult
+                )
+            shared.clear()
 
         summed = []
         due = []
-        late = []
-
-        def reductions(j):
-            if j < NGRP:
-                regroup_out_of_psum(j)
-            if 0 <= j - 3 < NGRP:
-                smallest(j - 3)
-            for t_lo, t_hi in due:
-                bank = st["s", t_lo // TB]
-                shares(
-                    bank[:, : TB * NCLS].rearrange("p (i k) -> p i k", k=NCLS),
-                    bank[:, TB * NCLS : TB * (NCLS + 1)],
-                    t_lo,
-                    t_hi,
-                )
-            due.clear()
-            for i in late:
-                gs = vector_sums(i)
-                nc.vector.tensor_reduce(out=tots[:, i * NT : (i + 1) * NT], in_=gs[:], axis=AX.X, op=ALU.add)
-                shares(gs[:], tots[:, i * NT : (i + 1) * NT], i * NT, (i + 1) * NT)
-            late.clear()
+        shared = []
 
         regroup_gpsimd(0)
         regroup_tensor(0)
-        for j in range(NGRP + 4):
-            if j < NGRP:
-                regroup(j, 0)
-            if 0 <= j - 1 < NGRP:
+        turn_tables()
+        for j in range(NGRP):
+            if j == 1:
+                quantise(0, "xg")
+            regroup(j, 0)
+            if j > 1:
                 quantise(j - 1, "xg")
-            if j < NGRP:
-                if j + 1 < NGRP:
-                    regroup_gpsimd(j + 1)
-                regroup(j, 1)
-                reductions(j)
-                if j + 1 < NGRP:
-                    regroup_tensor(j + 1)
-                square_scalar(j)
-                if j % UG == UG - 1 and 1 <= j // UG < IMAGES - RESIDENT:
-                    load(j // UG + RESIDENT)
+            if j + 1 < NGRP:
+                regroup_gpsimd(j + 1)
+            regroup(j, 1)
+            regroup_out_of_psum(j)
+            if j >= 3:
+                smallest(j - 3)
+            for t_hi in due:
+                bank_shares(t_hi)
+            due.clear()
+            if j == 1:
+                weights_product()
+            if j + 1 < NGRP:
+                regroup_tensor(j + 1)
+            square_scalar(j)
+            if j % UG == UG - 1 and 1 <= j // UG < IMAGES - RESIDENT:
+                load(j // UG + RESIDENT)
             if j == 0:
-                weights_scalar()
-            if 0 <= j - 1 < NGRP:
+                weights_exp_words()
+            if j >= 1:
                 quantise(j - 1, "x2")
             if j == 1:
-                weights_vector()
+                weights_words()
+                weights_constant()
                 weights_quantise()
-            if j < NGRP:
+            if j >= ALL_SCALAR:
                 square_vector(j)
+            divide()
             if j == 2:
                 constants()
-            if 0 <= j - 1 < NGRP:
+            if j >= 1:
                 products(j - 1)
-            if j >= NGRP:
-                reductions(j)
-            if 0 <= j - 2 < NGRP:
+            if j >= 2:
                 leave_psum(j - 2)
                 turn(j - 2)
             for q in summed:
                 pair_back(q)
                 t_hi = (q + 1) * PAIR * NT
                 if t_hi % TB == 0:
-                    due.append((t_hi - TB, t_hi))
-            summed = []
-            if 0 <= j - 3 < NGRP:
+                    due.append(t_hi)
+            summed.clear()
+            if j >= 3:
                 exponent(j - 3)
-                if j - 3 in V_SUMS:
-                    late.append(j - 3)
-                elif (j - 3) % PAIR == PAIR - 1:
+                if (j - 3) % PAIR == PAIR - 1:
                     pair_sums((j - 3) // PAIR)
                     summed.append((j - 3) // PAIR)
+        last = NGRP - 1
+        quantise_part(last, 0, "xg")
+        quantise_part(last, 0, "x2")
+        products(last, 0, LAST_PARTS)
+        leave_psum(last - 1)
+        turn(last - 1)
+        for q in summed:
+            pair_back(q)
+        smallest(last - 2)
+        exponent(last - 2)
+        quantise_part(last, 1, "xg")
+        smallest(last - 1)
+        quantise_part(last, 1, "x2")
+        pair_sums((last - 2) // PAIR)
+        leave_psum(last, 0, LAST_PARTS)
+        turn(last, 0, LAST_PARTS)
+        products(last, 1, LAST_PARTS)
+        exponent(last - 1)
+        smallest(last, 0, LAST_PARTS)
+        leave_psum(last, 1, LAST_PARTS)
+        turn(last, 1, LAST_PARTS)
+        pair_back((last - 2) // PAIR)
+        exponent(last, 0, LAST_PARTS)
+        vector_sums(last - 1)
+        smallest(last, 1, LAST_PARTS)
+        exponent(last, 1, LAST_PARTS)
+        bank_shares(min(V_SUMS) * NT)
+        vector_sums(last, 0, LAST_PARTS)
+        divide()
+        vector_sums(last, 1, LAST_PARTS)
+        vector_shares()
+        divide()
         resT = ps_t.tile([P, P], F32, tag="yT", name="resT")
         nc.tensor.transpose(resT[:], res[:], ident_f[:])
         res_sb = const.tile([P, P], F32, name="res_sb")

@@ -30,11 +30,13 @@ RESIDENT = 2
 HEAD_CUTS = (0, NG, 2 * NG, PIXELS)
 T_SHARE = 192
 G_SHARE = 160
-V_SHARE = 112
+GPSIMD_FROM = 4
+V_SHARE = 96
 ALL_SCALAR = 6
 V_SUMS = (NGRP - 2, NGRP - 1)
 assert (min(V_SUMS) * NT) % TB == 0
-LAST_PARTS = 2
+LAST_CUTS = (0, 2, 3, 4)
+WHOLE = (0, NT)
 
 FLOPS = 2 * 2 * (IMAGES * PIXELS) * CHANNELS * P
 
@@ -142,6 +144,7 @@ def tile_gmmoutlierdetector_t_kernel(tc, feats, means, log_vars, log_weights, ou
         ybias = const.tile([P, 1], F32, name="ybias")
         tops = const.tile([P, P], F32, name="tops")
         gs = const.tile([P, len(V_SUMS) * NT, NCLS], F32, name="gs")
+        late_tots = const.tile([P, len(V_SUMS) * NT], F32, name="late_tots")
         res = const.tile([P, P], F32, name="res")
 
         def weights_exp():
@@ -198,21 +201,22 @@ def tile_gmmoutlierdetector_t_kernel(tc, feats, means, log_vars, log_weights, ou
         V_END = NG - T_SHARE - G_SHARE
         G_END = NG - T_SHARE
 
+        def new_regrouped(j):
+            st["xg", j] = xgp.tile([P, G, NG, PACK], BF16, tag="xg", name="xg", align_bytes=64)
+
         def regroup_gpsimd(j):
-            xg = xgp.tile([P, G, NG, PACK], BF16, tag="xg", name="xg", align_bytes=64)
             piece, a = rows(j)
             nc.gpsimd.tensor_scalar(
-                out=xg[:, G - 1, V_END:G_END, :],
+                out=st["xg", j][:, G - 1, V_END:G_END, :],
                 in0=piece[:, G - 1, :, a + V_END : a + G_END].rearrange("p t n -> p n t"),
                 scalar1=1.0,
                 scalar2=0.0,
                 op0=ALU.mult,
                 op1=ALU.add,
             )
-            st["xg", j] = xg
 
         def regroup(j, g):
-            n = V_END if g == G - 1 else NG
+            n = NG if g == 0 else V_END if j >= GPSIMD_FROM else G_END
             nc.vector.tensor_copy(
                 out=st["xg", j][:, g, :n, :].rearrange("p (c i) t -> p c t i", i=4), in_=raw_view(j, g)[:, : n // 4]
             )
@@ -274,29 +278,29 @@ def tile_gmmoutlierdetector_t_kernel(tc, feats, means, log_vars, log_weights, ou
             )
             st[what + "q", j] = (codes, scales)
 
-        def quantise_part(j, h, what):
-            if h == 0:
+        def quantise_part(j, what, part):
+            n0, n1 = part[0] * P, part[1] * P
+            if n0 == 0:
                 codes = work.tile([P, G * NG], U32, tag=what + "c", name="codes", align_bytes=64)
                 scales = work.tile([P, G * NG], U8, tag=what + "s", name="scales", align_bytes=64)
                 st[what + "q", j] = (codes, scales)
             codes, scales = st[what + "q", j]
-            n = NG // LAST_PARTS
             for g in range(G):
-                c = slice(g * NG + h * n, g * NG + (h + 1) * n)
+                c = slice(g * NG + n0, g * NG + n1)
                 nc.vector.quantize_mx(
                     out=codes[:, c].bitcast(FP8X4),
                     scales=scales[:, c],
-                    in_=st[what, j][:, g, h * n : (h + 1) * n, :].rearrange("p n t -> p (n t)"),
+                    in_=st[what, j][:, g, n0:n1, :].rearrange("p n t -> p (n t)"),
                 )
 
-        def products(j, h=0, parts=1):
-            n = NG // parts
-            acc = ps_acc.tile([P, n], F32, tag="acc", name="acc")
+        def products(j, part=WHOLE):
+            n0, n1 = part[0] * P, part[1] * P
+            acc = ps_acc.tile([P, n1 - n0], F32, tag="acc", name="acc")
             passes = [(1, g, "xgq") for g in range(G)] + [(0, g, "x2q") for g in range(G)]
             for idx, (o, g, what) in enumerate(passes):
                 codes, scales = st[what, j]
                 a = (o * G + g) * P
-                c = slice(g * NG + h * n, g * NG + (h + 1) * n)
+                c = slice(g * NG + n0, g * NG + n1)
                 nc.tensor.matmul_mx(
                     out=acc[:],
                     lhsT=wc[:, a : a + P].bitcast(FP8X4),
@@ -306,34 +310,37 @@ def tile_gmmoutlierdetector_t_kernel(tc, feats, means, log_vars, log_weights, ou
                     start=(idx == 0),
                     stop=(idx == len(passes) - 1),
                 )
-            st["acc", j, h] = acc
+            st["acc", j, part] = acc
 
-        def leave_psum(j, h=0, parts=1):
-            y = work.tile([P, NG // parts], F32, tag="y", name="y")
+        def leave_psum(j, part=WHOLE):
+            y = work.tile([P, (part[1] - part[0]) * P], F32, tag="y", name="y")
             nc.scalar.activation(
-                out=y[:], in_=st["acc", j, h][:], func=ACT.Identity, bias=ybias[:, 0:1], scale=0.5
+                out=y[:], in_=st["acc", j, part][:], func=ACT.Identity, bias=ybias[:, 0:1], scale=0.5
             )
-            st["y", j, h] = y
+            st["y", j, part] = y
 
-        def turn(j, h=0, parts=1):
+        def turn(j, part=WHOLE):
             order = ident_f if j in V_SUMS else perm
-            nt = NT // parts
+            nt = part[1] - part[0]
             yT = ps_t.tile([P, nt, P], F32, tag="yT", name="yT")
             for i in range(nt):
-                nc.tensor.transpose(yT[:, i, :], st["y", j, h][:, i * P : (i + 1) * P], order[:])
-            st["yT", j, h] = yT
+                nc.tensor.transpose(yT[:, i, :], st["y", j, part][:, i * P : (i + 1) * P], order[:])
+            st["yT", j, part] = yT
 
-        def smallest(j, h=0, parts=1):
-            mn = work.tile([P, NT // parts], F32, tag="mn", name="mn")
-            nc.vector.tensor_reduce(out=mn[:], in_=st["yT", j, h][:], axis=AX.X, op=ALU.min)
-            st["mn", j, h] = mn
+        def smallest(j, part=WHOLE):
+            mn = work.tile([P, part[1] - part[0]], F32, tag="mn", name="mn")
+            nc.vector.tensor_reduce(out=mn[:], in_=st["yT", j, part][:], axis=AX.X, op=ALU.min)
+            st["mn", j, part] = mn
 
-        def exponent(j, h=0, parts=1):
-            nt = NT // parts
-            yT = st["yT", j, h]
+        def exponent(j, part=WHOLE):
+            nt = part[1] - part[0]
+            yT = st["yT", j, part]
+            tots = [None] * nt
             if j in V_SUMS:
                 e = work.tile([P, nt, P], F32, tag="e", name="e")
-                st["e", j, h] = e
+                st["e", j, part] = e
+                t_lo = (j - V_SUMS[0]) * NT + part[0]
+                tots = [late_tots[:, t_lo + i : t_lo + i + 1] for i in range(nt)]
                 outs = [e[:, i, :] for i in range(nt)]
                 ins = [yT[:, i, :] for i in range(nt)]
             else:
@@ -346,8 +353,9 @@ def tile_gmmoutlierdetector_t_kernel(tc, feats, means, log_vars, log_weights, ou
                     out=outs[i],
                     in_=ins[i],
                     func=ACT.Exp,
-                    bias=st["mn", j, h][:, i : i + 1],
+                    bias=st["mn", j, part][:, i : i + 1],
                     scale=-1.0,
+                    accum_out=tots[i],
                 )
 
         def pair_sums(q):
@@ -381,19 +389,17 @@ def tile_gmmoutlierdetector_t_kernel(tc, feats, means, log_vars, log_weights, ou
                 stop=True,
             )
 
-        def vector_sums(j, h=0, parts=1):
-            t_lo = (j - V_SUMS[0]) * NT + h * NT // parts
+        def vector_sums(j, part=WHOLE):
+            t_lo = (j - V_SUMS[0]) * NT
             nc.vector.tensor_reduce(
-                out=gs[:, t_lo : t_lo + NT // parts, :],
-                in_=st["e", j, h][:].rearrange("p i (k m) -> p i k m", m=NCMP),
+                out=gs[:, t_lo + part[0] : t_lo + part[1], :],
+                in_=st["e", j, part][:].rearrange("p i (k m) -> p i k m", m=NCMP),
                 axis=AX.X,
                 op=ALU.add,
             )
 
         def vector_shares():
-            tots = const.tile([P, len(V_SUMS) * NT], F32, name="tots")
-            nc.vector.tensor_reduce(out=tots[:], in_=gs[:], axis=AX.X, op=ALU.add)
-            shares(gs[:], tots[:], V_SUMS[0] * NT)
+            shares(gs[:], late_tots[:], V_SUMS[0] * NT)
 
         def bank_shares(t_hi):
             bank = st["s", t_hi // TB - 1]
@@ -406,8 +412,8 @@ def tile_gmmoutlierdetector_t_kernel(tc, feats, means, log_vars, log_weights, ou
         def shares(sv, totals, t_lo):
             n = sv.shape[1]
             rec = work.tile([P, TB], F32, tag="rec", name="rec")
-            nc.vector.tensor_reduce(out=tops[:, t_lo : t_lo + n], in_=sv, axis=AX.X, op=ALU.max)
             nc.vector.reciprocal(out=rec[:, :n], in_=totals)
+            nc.vector.tensor_reduce(out=tops[:, t_lo : t_lo + n], in_=sv, axis=AX.X, op=ALU.max)
             shared.append((rec, t_lo, t_lo + n))
 
         def divide():
@@ -421,7 +427,7 @@ def tile_gmmoutlierdetector_t_kernel(tc, feats, means, log_vars, log_weights, ou
         due = []
         shared = []
 
-        regroup_gpsimd(0)
+        new_regrouped(0)
         regroup_tensor(0)
         turn_tables()
         for j in range(NGRP):
@@ -431,6 +437,8 @@ def tile_gmmoutlierdetector_t_kernel(tc, feats, means, log_vars, log_weights, ou
             if j > 1:
                 quantise(j - 1, "xg")
             if j + 1 < NGRP:
+                new_regrouped(j + 1)
+            if GPSIMD_FROM <= j + 1 < NGRP:
                 regroup_gpsimd(j + 1)
             regroup(j, 1)
             regroup_out_of_psum(j)
@@ -476,35 +484,44 @@ def tile_gmmoutlierdetector_t_kernel(tc, feats, means, log_vars, log_weights, ou
                     pair_sums((j - 3) // PAIR)
                     summed.append((j - 3) // PAIR)
         last = NGRP - 1
-        quantise_part(last, 0, "xg")
-        quantise_part(last, 0, "x2")
-        products(last, 0, LAST_PARTS)
+        a, b, c = zip(LAST_CUTS[:-1], LAST_CUTS[1:])
+        quantise_part(last, "xg", a)
+        quantise_part(last, "x2", a)
+        products(last, a)
         leave_psum(last - 1)
         turn(last - 1)
         for q in summed:
             pair_back(q)
         smallest(last - 2)
         exponent(last - 2)
-        quantise_part(last, 1, "xg")
+        quantise_part(last, "xg", b)
+        quantise_part(last, "x2", b)
         smallest(last - 1)
-        quantise_part(last, 1, "x2")
         pair_sums((last - 2) // PAIR)
-        leave_psum(last, 0, LAST_PARTS)
-        turn(last, 0, LAST_PARTS)
-        products(last, 1, LAST_PARTS)
+        leave_psum(last, a)
+        turn(last, a)
+        products(last, b)
+        quantise_part(last, "xg", c)
+        quantise_part(last, "x2", c)
         exponent(last - 1)
-        smallest(last, 0, LAST_PARTS)
-        leave_psum(last, 1, LAST_PARTS)
-        turn(last, 1, LAST_PARTS)
+        smallest(last, a)
+        leave_psum(last, b)
+        turn(last, b)
+        products(last, c)
         pair_back((last - 2) // PAIR)
-        exponent(last, 0, LAST_PARTS)
+        exponent(last, a)
         vector_sums(last - 1)
-        smallest(last, 1, LAST_PARTS)
-        exponent(last, 1, LAST_PARTS)
+        smallest(last, b)
+        leave_psum(last, c)
+        turn(last, c)
+        exponent(last, b)
         bank_shares(min(V_SUMS) * NT)
-        vector_sums(last, 0, LAST_PARTS)
+        smallest(last, c)
+        exponent(last, c)
+        vector_sums(last, a)
+        vector_sums(last, b)
         divide()
-        vector_sums(last, 1, LAST_PARTS)
+        vector_sums(last, c)
         vector_shares()
         divide()
         resT = ps_t.tile([P, P], F32, tag="yT", name="resT")

@@ -31,7 +31,7 @@ HEAD_CUTS = (0, NG, 2 * NG, PIXELS)
 T_SHARE = 192
 G_SHARE = 160
 GPSIMD_FROM = 4
-V_SHARE = 96
+V_SHARE = 112
 ALL_SCALAR = 6
 V_SUMS = (NGRP - 2, NGRP - 1)
 assert (min(V_SUMS) * NT) % TB == 0

from contextlib import ExitStack

import concourse.mybir as mybir
from concourse.masks import make_identity

F32 = mybir.dt.float32
BF16 = mybir.dt.bfloat16
U32 = mybir.dt.uint32
U8 = mybir.dt.uint8
FP8X4 = mybir.dt.float8_e4m3fn_x4
ACT = mybir.ActivationFunctionType
ALU = mybir.AluOpType
AX = mybir.AxisListType

P = 128
PACK = 4
IMAGES = 8
CHANNELS = 1024
PIXELS = 2048
G = CHANNELS // (P * PACK)
NG = 512
NT = NG // P
UG = PIXELS // NG
NGRP = IMAGES * UG
NCLS = 16
NCMP = 8
PAIR = 2
TB = 24
RESIDENT = 2
HEAD_CUTS = (0, NG, 2 * NG, PIXELS)
T_SHARE = 192
G_SHARE = 160
GPSIMD_FROM = 4
V_SHARE = 112
ALL_SCALAR = 6
V_SUMS = (NGRP - 2, NGRP - 1)
assert (min(V_SUMS) * NT) % TB == 0
LAST_CUTS = (0, 2, 3, 4)
WHOLE = (0, NT)

FLOPS = 2 * 2 * (IMAGES * PIXELS) * CHANNELS * P


def tile_gmmoutlierdetector_t_kernel(tc, feats, means, log_vars, log_weights, out):
    nc = tc.nc
    with ExitStack() as ctx:
        const = ctx.enter_context(tc.tile_pool(name="const", bufs=1))
        head = ctx.enter_context(tc.tile_pool(name="head", bufs=1))
        rawp = ctx.enter_context(tc.tile_pool(name="rawp", bufs=RESIDENT))
        work = ctx.enter_context(tc.tile_pool(name="work", bufs=3))
        xgp = ctx.enter_context(tc.tile_pool(name="xgp", bufs=2))
        ps_acc = ctx.enter_context(tc.psum_pool(name="ps_acc", bufs=2))
        ps_t = ctx.enter_context(tc.psum_pool(name="ps_t", bufs=3))
        ps_s = ctx.enter_context(tc.psum_pool(name="ps_s", bufs=1))
        ps_x = ctx.enter_context(tc.psum_pool(name="ps_x", bufs=1))
        ps_u = ctx.enter_context(tc.psum_pool(name="ps_u", bufs=1))
        ctx.enter_context(tc.manual_schedule())

        fv = feats.rearrange("b (g p t) h w -> b g p t (h w)", g=G, p=P, t=PACK)
        st = {}

        def load(u):
            if u == 0:
                st["raw", u] = []
                for lo, hi in zip(HEAD_CUTS[:-1], HEAD_CUTS[1:]):
                    piece = head.tile([P, G, PACK, hi - lo], BF16, name="piece%d" % lo)
                    for g in range(G):
                        for t in range(PACK):
                            nc.sync.dma_start(out=piece[:, g, t, :], in_=fv[u, g, :, t, lo:hi])
                    st["raw", u].append((lo, hi, piece))
                    if lo == 0:
                        nc.sync.dma_start(out=lv[:], in_=log_vars.rearrange("k m d -> (k m) d"))
                        nc.sync.dma_start(out=mu[:], in_=means.rearrange("k m d -> (k m) d"))
            else:
                raw = rawp.tile([P, G, PACK, PIXELS], BF16, tag="raw", name="raw")
                for g in range(G):
                    nc.sync.dma_start(out=raw[:, g], in_=fv[u, g])
                st["raw", u] = [(0, PIXELS, raw)]

        def raw_view(j, g):
            n0 = (j % UG) * NG
            lo, piece = [(lo, piece) for lo, hi, piece in st["raw", j // UG] if lo <= n0 < hi][0]
            return piece[:, g, :, n0 - lo : n0 - lo + NG].rearrange("p t (c i) -> p c t i", i=4)

        lv = const.tile([P, CHANNELS], BF16, name="lv")
        mu = const.tile([P, CHANNELS], BF16, name="mu")
        lw = const.tile([P, 1], BF16, name="lw")
        for u in range(1 + RESIDENT):
            load(u)

        ones = const.tile([P, 1], F32, name="ones")
        nc.vector.memset(ones[:], 1.0)
        warm = const.tile([P, 1], F32, name="warm")
        nc.scalar.activation(out=warm[:], in_=ones[:], func=ACT.Exp)

        ident_bf = const.tile([P, P], BF16, name="ident_bf")
        make_identity(nc, ident_bf[:])
        ident_f = const.tile([P, P], F32, name="ident_f")
        make_identity(nc, ident_f[:])
        center = const.tile([P, P], BF16, name="center")
        nc.vector.tensor_scalar(
            out=center[:], in0=ident_bf[:], scalar1=-1.0 / P, scalar2=None, op0=ALU.add
        )
        perm = const.tile([P, P], F32, name="perm")
        nc.vector.tensor_copy(
            out=perm[:].rearrange("p (m k) -> p m k", m=NCMP),
            in_=ident_f[:].rearrange("p (k m) -> p m k", m=NCMP),
        )

        tile_of = const.tile([P, PAIR * NT], F32, name="tile_of")
        nc.vector.tensor_reduce(
            out=tile_of[:], in_=ident_f[:].rearrange("p (i k) -> p i k", k=NCLS), axis=AX.X, op=ALU.add
        )

        turned = {}
        nblk = CHANNELS // P

        def turn_tables():
            for what, table in (("lv", lv), ("mu", mu)):
                tableT = ps_t.tile([P, G, PACK, P], BF16, tag="yT", name="tableT")
                rows = table[:].rearrange("c (g p t) -> c g t p", g=G, p=P, t=PACK)
                for g in range(G):
                    for t in range(PACK):
                        nc.tensor.transpose(tableT[:, g, t, :], rows[:, g, t, :], ident_bf[:])
                turned[what] = tableT
            cst_ps = ps_u.tile([P, 2, P], F32, tag="u", name="cst_ps")
            turned["cst"] = cst_ps
            for i in range(nblk):
                nc.tensor.matmul(
                    out=cst_ps[:, 0, :],
                    lhsT=center[:],
                    rhs=lv[:, i * P : (i + 1) * P],
                    start=(i == 0),
                    stop=(i == nblk - 1),
                )

        ivT = const.tile([P, G, PACK, P], F32, name="ivT")
        mivT = const.tile([P, G, PACK, P], F32, name="mivT")
        m2T = const.tile([P, G, PACK, P], F32, name="m2T")
        wg = const.tile([P, 2 * G, P, PACK], BF16, name="wg", align_bytes=64)
        wc = const.tile([P, 2 * G * P], U32, name="wc", align_bytes=64)
        ws = const.tile([P, 2 * G * P], U8, name="ws", align_bytes=64)
        csum = const.tile([P, 1], F32, name="csum")
        ybias = const.tile([P, 1], F32, name="ybias")
        tops = const.tile([P, P], F32, name="tops")
        gs = const.tile([P, len(V_SUMS) * NT, NCLS], F32, name="gs")
        late_tots = const.tile([P, len(V_SUMS) * NT], F32, name="late_tots")
        res = const.tile([P, P], F32, name="res")

        def weights_exp():
            nc.scalar.activation(out=ivT[:], in_=turned["lv"][:], func=ACT.Exp, scale=-1.0)

        def weights_exp_words():
            nc.scalar.activation(
                out=wg[:, 0:G], in_=turned["lv"][:].rearrange("p g t c -> p g c t"), func=ACT.Exp, scale=-1.0
            )
            with nc.allow_non_contiguous_dma(reason="128 log weights, one to a partition"):
                nc.scalar.dma_start(out=lw[:], in_=log_weights.rearrange("k (m o) -> (k m) o", o=1))

        def weights_product():
            nc.vector.tensor_tensor(out=mivT[:], in0=turned["mu"][:], in1=ivT[:], op=ALU.mult)

        def weights_words():
            nc.vector.tensor_scalar(
                out=wg[:, G : 2 * G],
                in0=mivT[:].rearrange("p g t c -> p g c t"),
                scalar1=-2.0,
                scalar2=None,
                op0=ALU.mult,
            )

        def weights_constant():
            nc.vector.tensor_tensor(out=m2T[:], in0=turned["mu"][:], in1=mivT[:], op=ALU.mult)
            for i in range(nblk):
                nc.tensor.matmul(
                    out=turned["cst"][:, 1, 0:1],
                    lhsT=m2T[:, i // PACK, i % PACK, :],
                    rhs=ones[:],
                    start=(i == 0),
                    stop=(i == nblk - 1),
                )

        def weights_quantise():
            nc.vector.quantize_mx(
                out=wc[:].bitcast(FP8X4), scales=ws[:], in_=wg[:].rearrange("p a c t -> p (a c t)")
            )

        def constants():
            nc.vector.tensor_reduce(
                out=csum[:], in_=turned["cst"][:].rearrange("p a c -> p (a c)")[:, : P + 1], axis=AX.X, op=ALU.add
            )
            nc.vector.scalar_tensor_tensor(
                out=ybias[:], in0=csum[:], scalar=0.5, in1=lw[:], op0=ALU.mult, op1=ALU.subtract
            )

        def rows(j):
            n0 = (j % UG) * NG
            lo, piece = [(lo, piece) for lo, hi, piece in st["raw", j // UG] if lo <= n0 < hi][0]
            return piece, n0 - lo

        V_END = NG - T_SHARE - G_SHARE
        G_END = NG - T_SHARE

        def new_regrouped(j):
            st["xg", j] = xgp.tile([P, G, NG, PACK], BF16, tag="xg", name="xg", align_bytes=64)

        def regroup_gpsimd(j):
            piece, a = rows(j)
            nc.gpsimd.tensor_scalar(
                out=st["xg", j][:, G - 1, V_END:G_END, :],
                in0=piece[:, G - 1, :, a + V_END : a + G_END].rearrange("p t n -> p n t"),
                scalar1=1.0,
                scalar2=0.0,
                op0=ALU.mult,
                op1=ALU.add,
            )

        def regroup(j, g):
            n = NG if g == 0 else V_END if j >= GPSIMD_FROM else G_END
            nc.vector.tensor_copy(
                out=st["xg", j][:, g, :n, :].rearrange("p (c i) t -> p c t i", i=4), in_=raw_view(j, g)[:, : n // 4]
            )

        def regroup_tensor(j):
            piece, a = rows(j)
            xp = ps_x.tile([P, T_SHARE, PACK], BF16, tag="xp", name="xp")
            for lo in range(0, T_SHARE, P):
                hi = min(lo + P, T_SHARE)
                nc.tensor.matmul(
                    out=xp[:, lo:hi, :].rearrange("p n t -> p (n t)"),
                    lhsT=ident_bf[:],
                    rhs=piece[:, G - 1, :, a + G_END + lo : a + G_END + hi].rearrange("p t n -> p n t"),
                    start=True,
                    stop=True,
                )
            st["xp", j] = xp

        def regroup_out_of_psum(j):
            nc.vector.tensor_copy(
                out=st["xg", j][:, G - 1, G_END:, :].rearrange("p n t -> p (n t)"),
                in_=st["xp", j][:].rearrange("p n t -> p (n t)"),
            )

        def square_scalar(j):
            x2 = work.tile([P, G, NG, PACK], BF16, tag="x2", name="x2", align_bytes=64)
            st["x2", j] = x2
            for g in range(G):
                n = NG - V_SHARE if g == 0 and j >= ALL_SCALAR else NG
                if j in (0, NGRP - 1):
                    nc.scalar.activation(
                        out=x2[:, g, :n, :].rearrange("p (c i) t -> p c t i", i=4),
                        in_=raw_view(j, g)[:, : n // 4],
                        func=ACT.Square,
                    )
                    if j == g == 0:
                        weights_exp()
                else:
                    nc.scalar.activation(
                        out=x2[:, g, :n, :].rearrange("p n t -> p (n t)"),
                        in_=st["xg", j][:, g, :n, :].rearrange("p n t -> p (n t)"),
                        func=ACT.Square,
                    )

        def square_vector(j):
            lo = NG - V_SHARE
            xv = st["xg", j][:, 0, lo:, :].rearrange("p n t -> p (n t)")
            nc.vector.tensor_tensor(
                out=st["x2", j][:, 0, lo:, :].rearrange("p n t -> p (n t)"), in0=xv, in1=xv, op=ALU.mult
            )

        def quantise(j, what):
            codes = work.tile([P, G * NG], U32, tag=what + "c", name="codes", align_bytes=64)
            scales = work.tile([P, G * NG], U8, tag=what + "s", name="scales", align_bytes=64)
            nc.vector.quantize_mx(
                out=codes[:].bitcast(FP8X4),
                scales=scales[:],
                in_=st[what, j][:].rearrange("p g n t -> p (g n t)"),
            )
            st[what + "q", j] = (codes, scales)

        def quantise_part(j, what, part):
            n0, n1 = part[0] * P, part[1] * P
            if n0 == 0:
                codes = work.tile([P, G * NG], U32, tag=what + "c", name="codes", align_bytes=64)
                scales = work.tile([P, G * NG], U8, tag=what + "s", name="scales", align_bytes=64)
                st[what + "q", j] = (codes, scales)
            codes, scales = st[what + "q", j]
            for g in range(G):
                c = slice(g * NG + n0, g * NG + n1)
                nc.vector.quantize_mx(
                    out=codes[:, c].bitcast(FP8X4),
                    scales=scales[:, c],
                    in_=st[what, j][:, g, n0:n1, :].rearrange("p n t -> p (n t)"),
                )

        def products(j, part=WHOLE):
            n0, n1 = part[0] * P, part[1] * P
            acc = ps_acc.tile([P, n1 - n0], F32, tag="acc", name="acc")
            passes = [(1, g, "xgq") for g in range(G)] + [(0, g, "x2q") for g in range(G)]
            for idx, (o, g, what) in enumerate(passes):
                codes, scales = st[what, j]
                a = (o * G + g) * P
                c = slice(g * NG + n0, g * NG + n1)
                nc.tensor.matmul_mx(
                    out=acc[:],
                    lhsT=wc[:, a : a + P].bitcast(FP8X4),
                    lhsT_scale=ws[:, a : a + P],
                    rhs=codes[:, c].bitcast(FP8X4),
                    rhs_scale=scales[:, c],
                    start=(idx == 0),
                    stop=(idx == len(passes) - 1),
                )
            st["acc", j, part] = acc

        def leave_psum(j, part=WHOLE):
            y = work.tile([P, (part[1] - part[0]) * P], F32, tag="y", name="y")
            nc.scalar.activation(
                out=y[:], in_=st["acc", j, part][:], func=ACT.Identity, bias=ybias[:, 0:1], scale=0.5
            )
            st["y", j, part] = y

        def turn(j, part=WHOLE):
            order = ident_f if j in V_SUMS else perm
            nt = part[1] - part[0]
            yT = ps_t.tile([P, nt, P], F32, tag="yT", name="yT")
            for i in range(nt):
                nc.tensor.transpose(yT[:, i, :], st["y", j, part][:, i * P : (i + 1) * P], order[:])
            st["yT", j, part] = yT

        def smallest(j, part=WHOLE):
            mn = work.tile([P, part[1] - part[0]], F32, tag="mn", name="mn")
            nc.vector.tensor_reduce(out=mn[:], in_=st["yT", j, part][:], axis=AX.X, op=ALU.min)
            st["mn", j, part] = mn

        def exponent(j, part=WHOLE):
            nt = part[1] - part[0]
            yT = st["yT", j, part]
            tots = [None] * nt
            if j in V_SUMS:
                e = work.tile([P, nt, P], F32, tag="e", name="e")
                st["e", j, part] = e
                t_lo = (j - V_SUMS[0]) * NT + part[0]
                tots = [late_tots[:, t_lo + i : t_lo + i + 1] for i in range(nt)]
                outs = [e[:, i, :] for i in range(nt)]
                ins = [yT[:, i, :] for i in range(nt)]
            else:
                if j % PAIR == 0:
                    st["eb", j // PAIR] = work.tile([P, NCMP, PAIR * NT, NCLS], F32, tag="eb", name="eb")
                outs = [st["eb", j // PAIR][:, :, (j % PAIR) * NT + i, :] for i in range(nt)]
                ins = [yT[:, i, :].rearrange("p (m k) -> p m k", m=NCMP) for i in range(nt)]
            for i in range(nt):
                nc.scalar.activation(
                    out=outs[i],
                    in_=ins[i],
                    func=ACT.Exp,
                    bias=st["mn", j, part][:, i : i + 1],
                    scale=-1.0,
                    accum_out=tots[i],
                )

        def pair_sums(q):
            sT = ps_u.tile([P, P], F32, tag="u", name="sT")
            for m in range(NCMP):
                nc.tensor.matmul(
                    out=sT[:],
                    lhsT=st["eb", q][:, m].rearrange("p i k -> p (i k)"),
                    rhs=ident_f[:],
                    start=(m == 0),
                    stop=(m == NCMP - 1),
                    is_transpose=True,
                )
            st["sT", q] = sT

        def pair_back(q):
            sT_sb = work.tile([P, P], F32, tag="sT_sb", name="sT_sb")
            nc.scalar.copy(out=sT_sb[:], in_=st["sT", q][:])
            t_lo = q * PAIR * NT
            if t_lo % TB == 0:
                st["s", t_lo // TB] = ps_s.tile([P, NG], F32, tag="s", name="s_ps")
            slot = t_lo % TB
            nc.tensor.transpose(
                st["s", t_lo // TB][:, slot * NCLS : (slot + PAIR * NT) * NCLS], sT_sb[:], ident_f[:]
            )
            nc.tensor.matmul(
                out=st["s", t_lo // TB][:, TB * NCLS + slot : TB * NCLS + slot + PAIR * NT],
                lhsT=sT_sb[:],
                rhs=tile_of[:],
                start=True,
                stop=True,
            )

        def vector_sums(j, part=WHOLE):
            t_lo = (j - V_SUMS[0]) * NT
            nc.vector.tensor_reduce(
                out=gs[:, t_lo + part[0] : t_lo + part[1], :],
                in_=st["e", j, part][:].rearrange("p i (k m) -> p i k m", m=NCMP),
                axis=AX.X,
                op=ALU.add,
            )

        def vector_shares():
            shares(gs[:], late_tots[:], V_SUMS[0] * NT)

        def bank_shares(t_hi):
            bank = st["s", t_hi // TB - 1]
            shares(
                bank[:, : TB * NCLS].rearrange("p (i k) -> p i k", k=NCLS),
                bank[:, TB * NCLS : TB * (NCLS + 1)],
                t_hi - TB,
            )

        def shares(sv, totals, t_lo):
            n = sv.shape[1]
            rec = work.tile([P, TB], F32, tag="rec", name="rec")
            nc.vector.reciprocal(out=rec[:, :n], in_=totals)
            nc.vector.tensor_reduce(out=tops[:, t_lo : t_lo + n], in_=sv, axis=AX.X, op=ALU.max)
            shared.append((rec, t_lo, t_lo + n))

        def divide():
            for rec, t_lo, t_hi in shared:
                nc.vector.tensor_tensor(
                    out=res[:, t_lo:t_hi], in0=tops[:, t_lo:t_hi], in1=rec[:, : t_hi - t_lo], op=ALU.mult
                )
            shared.clear()

        summed = []
        due = []
        shared = []

        new_regrouped(0)
        regroup_tensor(0)
        turn_tables()
        for j in range(NGRP):
            if j == 1:
                quantise(0, "xg")
            regroup(j, 0)
            if j > 1:
                quantise(j - 1, "xg")
            if j + 1 < NGRP:
                new_regrouped(j + 1)
            if GPSIMD_FROM <= j + 1 < NGRP:
                regroup_gpsimd(j + 1)
            regroup(j, 1)
            regroup_out_of_psum(j)
            if j >= 3:
                smallest(j - 3)
            for t_hi in due:
                bank_shares(t_hi)
            due.clear()
            if j == 1:
                weights_product()
            if j + 1 < NGRP:
                regroup_tensor(j + 1)
            square_scalar(j)
            if j % UG == UG - 1 and 1 <= j // UG < IMAGES - RESIDENT:
                load(j // UG + RESIDENT)
            if j == 0:
                weights_exp_words()
            if j >= 1:
                quantise(j - 1, "x2")
            if j == 1:
                weights_words()
                weights_constant()
                weights_quantise()
            if j >= ALL_SCALAR:
                square_vector(j)
            divide()
            if j == 2:
                constants()
            if j >= 1:
                products(j - 1)
            if j >= 2:
                leave_psum(j - 2)
                turn(j - 2)
            for q in summed:
                pair_back(q)
                t_hi = (q + 1) * PAIR * NT
                if t_hi % TB == 0:
                    due.append(t_hi)
            summed.clear()
            if j >= 3:
                exponent(j - 3)
                if (j - 3) % PAIR == PAIR - 1:
                    pair_sums((j - 3) // PAIR)
                    summed.append((j - 3) // PAIR)
        last = NGRP - 1
        a, b, c = zip(LAST_CUTS[:-1], LAST_CUTS[1:])
        quantise_part(last, "xg", a)
        quantise_part(last, "x2", a)
        products(last, a)
        leave_psum(last - 1)
        turn(last - 1)
        for q in summed:
            pair_back(q)
        smallest(last - 2)
        exponent(last - 2)
        quantise_part(last, "xg", b)
        quantise_part(last, "x2", b)
        smallest(last - 1)
        pair_sums((last - 2) // PAIR)
        leave_psum(last, a)
        turn(last, a)
        products(last, b)
        quantise_part(last, "xg", c)
        quantise_part(last, "x2", c)
        exponent(last - 1)
        smallest(last, a)
        leave_psum(last, b)
        turn(last, b)
        products(last, c)
        pair_back((last - 2) // PAIR)
        exponent(last, a)
        vector_sums(last - 1)
        smallest(last, b)
        leave_psum(last, c)
        turn(last, c)
        exponent(last, b)
        bank_shares(min(V_SUMS) * NT)
        smallest(last, c)
        exponent(last, c)
        vector_sums(last, a)
        vector_sums(last, b)
        divide()
        vector_sums(last, c)
        vector_shares()
        divide()
        resT = ps_t.tile([P, P], F32, tag="yT", name="resT")
        nc.tensor.transpose(resT[:], res[:], ident_f[:])
        res_sb = const.tile([P, P], F32, name="res_sb")
        nc.vector.tensor_scalar(
            out=res_sb[:], in0=resT[:], scalar1=-1.0, scalar2=1.0, op0=ALU.mult, op1=ALU.add
        )
        nc.sync.dma_start(out=out.rearrange("b (x y) w -> (b x) (y w)", y=2), in_=res_sb[:])
